import numpy as np
import ml_dtypes


def mxq(x, axis, fmt="e4m3"):
    dtype, down = {"e4m3": (ml_dtypes.float8_e4m3fn, 7), "e5m2": (ml_dtypes.float8_e5m2, 14)}[fmt]
    v = np.moveaxis(np.asarray(x, np.float32).astype(ml_dtypes.bfloat16).astype(np.float64), axis, -1)
    blocks = v.reshape(v.shape[:-1] + (-1, 32))
    amax = np.abs(blocks).max(-1, keepdims=True)
    byte = np.maximum(np.where(amax > 0, np.frexp(amax)[1] - 1 + 127, 0) - down, 1)
    scale = np.exp2(byte - 127.0)
    codes = (blocks / scale).astype(np.float32).astype(dtype).astype(np.float64)
    return np.moveaxis((codes * scale).reshape(v.shape), -1, axis)


WIDE = False


def mx_kscale(k):
    if not WIDE:
        return np.ones(k)
    levels = np.array([10, -10, 5, -5, 0])
    if k % 512:
        return np.exp2(np.random.permutation(np.resize(levels, k // 32))).repeat(32)
    a = np.empty((k // 512, 16))
    for p in range(k // 512):
        a[p, :8] = np.random.permutation(np.resize(levels, 8))
        for g in range(8):
            far = levels[np.abs(levels - a[p, g]) >= 10]
            a[p, g + 8] = far[np.random.randint(len(far))]
    return np.exp2(a.ravel()).repeat(32)


BF16 = ml_dtypes.bfloat16


def bf(x):
    return np.asarray(x, np.float32).astype(BF16)


def f64(x):
    return np.asarray(x).astype(np.float64)


T, B, D, U, V, E = 4, 256, 512, 512, 512, 8
G = 2 * E
GS = (T + 1) * E


def softmax(v):
    e = np.exp(v - v.max(-1, keepdims=True))
    return e / e.sum(-1, keepdims=True)


def draw0():
    rn = np.random.standard_normal
    s = mx_kscale(D)
    return {
        "x": bf(rn((B, D)) * s),
        "ews0": bf(rn((D, U, E)) / np.sqrt(D) / s[:, None, None]),
        "ebs0": bf(rn((U, E)) * 0.5),
        "ew0": bf(rn((T, D, U, E)) / np.sqrt(D) / s[None, :, None, None]),
        "eb0": bf(rn((T, U, E)) * 0.5),
        "gate_pre0": bf(rn((T, B, G))),
        "gb0": bf(rn((T, G)) * 0.5),
        "sgate_pre": bf(rn((B, GS))),
        "gbs": bf(rn((GS,)) * 0.5),
    }


def core(x, ews0, ebs0, ew0, eb0, gate_pre0, gb0, sgate_pre, gbs):
    xq = mxq(f64(x), 1, "e4m3")
    es = np.maximum((xq @ mxq(f64(ews0).reshape(D, U * E), 0, "e4m3")).reshape(B, U, E) + f64(ebs0), 0.0)
    et = np.maximum((xq @ mxq(f64(ew0).reshape(T, D, U * E), 1, "e4m3")).reshape(T, B, U, E) + f64(eb0)[:, None], 0.0)
    g = softmax(f64(gate_pre0) + f64(gb0)[:, None])
    comb = np.concatenate([et, np.broadcast_to(es, et.shape)], axis=-1)
    task_out = (comb * g[:, :, None, :]).sum(-1)
    gs = softmax(f64(sgate_pre) + f64(gbs))
    all_exp = np.concatenate([np.moveaxis(et, 0, 2).reshape(B, U, T * E), es], axis=-1)
    share_out = (all_exp * gs[:, None, :]).sum(-1)
    return task_out, share_out


def e4m3fn_bytes(y):
    return np.clip(np.asarray(y, np.float64), -448.0, 448.0).astype(np.float32).astype(ml_dtypes.float8_e4m3fn).view(np.uint8)


def e4m3fn_values(b):
    return np.asarray(b, np.uint8).view(ml_dtypes.float8_e4m3fn).astype(np.float64)


def setup_inputs():
    d = draw0()
    x0 = np.asarray(d['ew0']).astype(np.float64)
    s = (np.max(np.abs(x0), axis=(0, 2, 3), keepdims=True) / 448.0).astype(np.float32)
    out = {}
    for k, v in d.items():
        if k == 'ew0':
            out['ew0_bytes'] = e4m3fn_bytes(x0 / s.astype(np.float64))
            out['ew0_scale'] = s
        else:
            out[k] = v
    return out


def reference(x, ews0, ebs0, ew0_bytes, ew0_scale, eb0, gate_pre0, gb0, sgate_pre, gbs):
    return core(x, ews0, ebs0, e4m3fn_values(ew0_bytes) * ew0_scale.astype(np.float64), eb0, gate_pre0, gb0, sgate_pre, gbs)

@@ -1,0 +1,283 @@
+from contextlib import ExitStack
+
+import concourse.mybir as mybir
+from concourse.masks import make_identity
+
+T, B, D, U, E = 4, 256, 512, 512, 8
+FLOPS = 2 * B * D * (T + 1) * U * E
+
+F32 = mybir.dt.float32
+BF16 = mybir.dt.bfloat16
+U32 = mybir.dt.uint32
+U8 = mybir.dt.uint8
+FP8 = mybir.dt.float8_e4m3fn
+FP8X4 = mybir.dt.float8_e4m3fn_x4
+ACT = mybir.ActivationFunctionType
+ALU = mybir.AluOpType
+AX = mybir.AxisListType
+
+P = 128
+PACK = 4
+NG = T + 1
+UC = U // P
+NB = 16
+BC = B // NB
+SLAB = P * E
+NSLOT = 13
+GROUP_ORDER = (T, 0, 1, 2, 3)
+
+
+def tile_plelayer_pa_kernel(
+    tc, x, ews0, ebs0, ew0_bytes, ew0_scale, eb0, gate_pre0, gb0, sgate_pre, gbs, out_0, out_1
+):
+    nc = tc.nc
+    with ExitStack() as ctx:
+        const = ctx.enter_context(tc.tile_pool(name="const", bufs=1))
+        stage = ctx.enter_context(tc.tile_pool(name="stage", bufs=2))
+        psum = ctx.enter_context(tc.psum_pool(name="psum", bufs=2))
+
+        ident = const.tile([P, P], F32, name="ident")
+        make_identity(nc, ident[:])
+
+        x_sb = const.tile([P, 2, D], BF16, name="x_sb")
+        nc.sync.dma_start(out=x_sb[:], in_=x.rearrange("(h p) d -> p h d", p=P))
+        sc = const.tile([P, PACK], F32, name="sc")
+        nc.sync.dma_start(out=sc[:], in_=ew0_scale.rearrange("o (p j) a b -> p (o j a b)", j=PACK))
+
+        xt = psum.tile([P, 2, 2, P], F32, name="xt", tag="misc")
+        for h in range(2):
+            words = x_sb[:, h, :].bitcast(F32)
+            for w in range(2):
+                nc.tensor.transpose(xt[:, h, w, :], words[:, w : D // 2 : 2], ident[:])
+        xg = const.tile([P, PACK * B], BF16, name="xg", align_bytes=64)
+        nc.vector.tensor_copy(
+            out=xg[:].bitcast(F32).rearrange("p (h r w) -> p h r w", h=2, w=2),
+            in_=xt[:].rearrange("p h w r -> p h r w"),
+        )
+        xcodes = const.tile([P, B], U32, name="xcodes", align_bytes=64)
+        xscl = const.tile([P, B], U8, name="xscl", align_bytes=64)
+        nc.vector.quantize_mx(out=xcodes[:].bitcast(FP8X4), scales=xscl[:], in_=xg[:])
+
+        bias_bf = const.tile([P, NG, UC, E], BF16, name="bias_bf")
+        for t in range(T):
+            nc.gpsimd.dma_start(out=bias_bf[:, t, :, :], in_=eb0[t].rearrange("(c p) e -> p c e", p=P))
+        nc.gpsimd.dma_start(out=bias_bf[:, T, :, :], in_=ebs0.rearrange("(c p) e -> p c e", p=P))
+        bias_u = const.tile([P, NG, UC, E], F32, name="bias_u")
+        nc.gpsimd.tensor_copy(out=bias_u[:], in_=bias_bf[:])
+
+        lg_t = const.tile([P, 2, 64], BF16, name="lg_t")
+        for h in range(2):
+            nc.gpsimd.dma_start(
+                out=lg_t[:, h, :].rearrange("p (t k) -> p t k", t=T),
+                in_=gate_pre0[:, h * P : (h + 1) * P, :].rearrange("t p k -> p t k"),
+            )
+        lg_s = const.tile([P, 2, 40], BF16, name="lg_s")
+        nc.gpsimd.dma_start(out=lg_s[:], in_=sgate_pre.rearrange("(h p) k -> p h k", p=P))
+        gb_t = const.tile([P, 64], BF16, name="gb_t")
+        nc.gpsimd.dma_start(out=gb_t[:], in_=gb0.rearrange("t k -> (t k)").partition_broadcast(P))
+        gb_s = const.tile([P, 40], BF16, name="gb_s")
+        nc.gpsimd.dma_start(out=gb_s[:], in_=gbs.partition_broadcast(P))
+
+        dall = const.tile([P, BC, NSLOT, NB], F32, name="dall")
+
+        def build_gates():
+            gl = const.tile([P, 2, 104], F32, name="gl")
+            nc.vector.tensor_tensor(
+                out=gl[:, :, 0:64], in0=lg_t[:], in1=gb_t[:].unsqueeze(1).to_broadcast([P, 2, 64]), op=ALU.add
+            )
+            nc.vector.tensor_tensor(
+                out=gl[:, :, 64:104], in0=lg_s[:], in1=gb_s[:].unsqueeze(1).to_broadcast([P, 2, 40]), op=ALU.add
+            )
+            task_view = gl[:, :, 0:64].rearrange("p h (t k) -> p h t k", t=T)
+            share_view = gl[:, :, 64:104]
+            mx = const.tile([P, 2, 5], F32, name="mx")
+            nc.vector.tensor_reduce(out=mx[:, :, 0:4], in_=task_view, axis=AX.X, op=ALU.max)
+            nc.vector.tensor_reduce(out=mx[:, :, 4:5], in_=share_view, axis=AX.X, op=ALU.max)
+            nc.vector.tensor_tensor(
+                out=task_view, in0=task_view, in1=mx[:, :, 0:4].unsqueeze(3).to_broadcast([P, 2, T, 16]), op=ALU.subtract
+            )
+            nc.vector.tensor_tensor(
+                out=share_view, in0=share_view, in1=mx[:, :, 4:5].to_broadcast([P, 2, 40]), op=ALU.subtract
+            )
+            nc.scalar.activation(out=gl[:], in_=gl[:], func=ACT.Exp)
+            sm = const.tile([P, 2, 5], F32, name="sm")
+            nc.vector.tensor_reduce(out=sm[:, :, 0:4], in_=task_view, axis=AX.X, op=ALU.add)
+            nc.vector.tensor_reduce(out=sm[:, :, 4:5], in_=share_view, axis=AX.X, op=ALU.add)
+            rc = const.tile([P, 2, 5], F32, name="rc")
+            nc.vector.reciprocal(out=rc[:], in_=sm[:])
+            nc.vector.tensor_tensor(
+                out=task_view, in0=task_view, in1=rc[:, :, 0:4].unsqueeze(3).to_broadcast([P, 2, T, 16]), op=ALU.mult
+            )
+            nc.vector.tensor_tensor(
+                out=share_view, in0=share_view, in1=rc[:, :, 4:5].to_broadcast([P, 2, 40]), op=ALU.mult
+            )
+            mask = const.tile([P, NB], F32, name="mask")
+            nc.vector.tensor_reduce(
+                out=mask[:], in_=ident[:].rearrange("p (c b) -> p b c", b=NB), axis=AX.X, op=ALU.add
+            )
+            mask4 = mask[:].unsqueeze(1).unsqueeze(1).to_broadcast([P, T, E, NB])
+            for h in range(2):
+                fm = const.tile([P, NSLOT, E, NB], F32, name="fm", tag="fm", bufs=2)
+                halves = gl[:, h, 0:64].rearrange("p (t s e) -> p t s e", t=T, s=2)
+                own = halves[:, :, 0, :].unsqueeze(3).to_broadcast([P, T, E, NB])
+                shared = halves[:, :, 1, :].unsqueeze(3).to_broadcast([P, T, E, NB])
+                sh_t = gl[:, h, 64:96].rearrange("p (t e) -> p t e", t=T).unsqueeze(3).to_broadcast([P, T, E, NB])
+                sh_s = gl[:, h, 96:104].unsqueeze(2).to_broadcast([P, E, NB])
+                nc.vector.tensor_tensor(out=fm[:, 0:4, :, :], in0=shared, in1=mask4, op=ALU.mult)
+                nc.vector.tensor_tensor(
+                    out=fm[:, 4, :, :], in0=sh_s, in1=mask[:].unsqueeze(1).to_broadcast([P, E, NB]), op=ALU.mult
+                )
+                nc.vector.tensor_tensor(out=fm[:, 5:NSLOT:2, :, :], in0=own, in1=mask4, op=ALU.mult)
+                nc.vector.tensor_tensor(out=fm[:, 6:NSLOT:2, :, :], in0=sh_t, in1=mask4, op=ALU.mult)
+                for s0 in range(0, NSLOT, 4):
+                    n = min(4, NSLOT - s0)
+                    dps = psum.tile([P, 4, P], F32, name="dps", tag="misc")
+                    for i in range(n):
+                        nc.tensor.transpose(
+                            dps[:, i, :], fm[:, s0 + i, :, :].rearrange("p e b -> p (e b)"), ident[:]
+                        )
+                    nc.vector.tensor_copy(
+                        out=dall[:, 8 * h : 8 * h + 8, s0 : s0 + n, :].rearrange("p c s b -> p s c b"),
+                        in_=dps[:, 0:n, :].rearrange("p s (c b) -> p s c b", b=NB),
+                    )
+
+        units = [(uc, g) for uc in range(UC) for g in GROUP_ORDER]
+        n_units = len(units)
+        raw, planes, grouped, codes, scales, relu_out = {}, {}, {}, {}, {}, {}
+        turned = {}
+
+        def load(i):
+            uc, g = units[i]
+            cols = slice(uc * SLAB, (uc + 1) * SLAB)
+            if g == T:
+                pl = stage.tile([P, PACK, SLAB], BF16, name="planes", tag="planes", bufs=3)
+                nc.sync.dma_start(out=pl[:], in_=ews0.rearrange("(p j) u e -> p j (u e)", j=PACK)[:, :, cols])
+                planes[i] = pl
+            else:
+                wb = stage.tile([P, PACK, SLAB], U8, name="wbytes", tag="wbytes", bufs=3)
+                nc.sync.dma_start(out=wb[:], in_=ew0_bytes[g].rearrange("(p j) u e -> p j (u e)", j=PACK)[:, :, cols])
+                raw[i] = wb
+
+        def widen(i):
+            if units[i][1] == T:
+                return
+            wb = raw[i]
+            pl = stage.tile([P, PACK, SLAB], BF16, name="planes", tag="planes", bufs=3)
+            for j in range(PACK):
+                nc.scalar.activation(
+                    out=pl[:, j, :], in_=wb[:, j, :].bitcast(FP8), func=ACT.Copy, scale=sc[:, j : j + 1]
+                )
+            planes[i] = pl
+
+        def interleave(i):
+            pl = planes[i]
+            gr = stage.tile([P, PACK * SLAB], BF16, name="grp", tag="grp", bufs=2, align_bytes=64)
+            dst = gr[:].rearrange("p (e u j) -> p u e j", e=E, j=PACK)
+            src = pl[:].rearrange("p j (u e) -> p u e j", e=E)
+            for e0 in (0, 4):
+                nc.vector.tensor_copy(out=dst[:, :, e0 : e0 + 4, :], in_=src[:, :, e0 : e0 + 4, :])
+            grouped[i] = gr
+
+        def quantize(i):
+            gr = grouped[i]
+            cd = stage.tile([P, SLAB], U32, name="wcodes", tag="wcodes", bufs=2, align_bytes=64)
+            sl = stage.tile([P, SLAB], U8, name="wscl", tag="wscl", bufs=2, align_bytes=64)
+            nc.vector.quantize_mx(out=cd[:].bitcast(FP8X4), scales=sl[:], in_=gr[:])
+            codes[i], scales[i] = cd, sl
+
+        def experts(i):
+            uc, g = units[i]
+            cd, sl = codes[i], scales[i]
+            hs = stage.tile([P, BC, E, NB], F32, name="hs", tag="hs", bufs=2)
+            for e0 in range(0, E, 2):
+                z = psum.tile([P, 2, B], F32, name="z", tag="z")
+                for k in range(2):
+                    cols = slice((e0 + k) * P, (e0 + k + 1) * P)
+                    nc.tensor.matmul_mx(
+                        out=z[:, k, :],
+                        lhsT=cd[:, cols].bitcast(FP8X4),
+                        lhsT_scale=sl[:, cols],
+                        rhs=xcodes[:].bitcast(FP8X4),
+                        rhs_scale=xscl[:],
+                        start=True,
+                        stop=True,
+                    )
+                for k in range(2):
+                    e = e0 + k
+                    nc.scalar.activation(
+                        out=hs[:, :, e, :],
+                        in_=z[:, k, :].rearrange("p (c b) -> p c b", b=NB),
+                        func=ACT.Relu,
+                        bias=bias_u[:, g, uc, e : e + 1],
+                        scale=1.0,
+                    )
+            relu_out[i] = hs
+
+        def turn(i):
+            uc, g = units[i]
+            hs = relu_out[i]
+            ht = stage.tile([P, BC, P], F32, name="ht%d" % g, tag="ht%d" % g, bufs=2)
+            for q in range(4):
+                tp = psum.tile([P, 4, P], F32, name="tp", tag="tp")
+                for k in range(4):
+                    nc.tensor.transpose(tp[:, k, :], hs[:, 4 * q + k, :, :].rearrange("p e b -> p (e b)"), ident[:])
+                nc.vector.tensor_copy(out=ht[:, 4 * q : 4 * q + 4, :], in_=tp[:])
+            turned[g] = ht
+
+        def gate_and_store(uc):
+            ot = stage.tile([P, NG, B], F32, name="ot", tag="ot", bufs=2)
+            for q in range(4):
+                o = psum.tile([P, 4, NG, NB], F32, name="o", tag="o")
+                for k in range(4):
+                    bc = 4 * q + k
+                    nc.tensor.matmul(
+                        out=o[:, k, :, :].rearrange("p j b -> p (j b)"),
+                        lhsT=turned[T][:, bc, :],
+                        rhs=dall[:, bc, 0:NG, :].rearrange("p s b -> p (s b)"),
+                        start=True,
+                        stop=False,
+                    )
+                    for t in range(T):
+                        nc.tensor.matmul(
+                            out=o[:, k, t : NG : T - t, :],
+                            lhsT=turned[t][:, bc, :],
+                            rhs=dall[:, bc, 5 + 2 * t : 7 + 2 * t, :],
+                            start=False,
+                            stop=(t == T - 1),
+                        )
+                nc.vector.tensor_copy(
+                    out=ot[:, :, 64 * q : 64 * q + 64].rearrange("p j (k b) -> p k j b", b=NB), in_=o[:]
+                )
+            ucols = slice(uc * P, (uc + 1) * P)
+            for h in range(2):
+                rows = slice(h * P, (h + 1) * P)
+                fp = psum.tile([P, T, P], F32, name="fp", tag="misc")
+                for t in range(T):
+                    nc.tensor.transpose(fp[:, t, :], ot[:, t, rows], ident[:])
+                res = stage.tile([P, T, P], F32, name="res", tag="res", bufs=2)
+                nc.vector.tensor_copy(out=res[:], in_=fp[:])
+                nc.sync.dma_start(out=out_0[:, rows, ucols].rearrange("t p u -> p t u"), in_=res[:])
+            fs = psum.tile([P, 2, P], F32, name="fs", tag="misc")
+            for h in range(2):
+                nc.tensor.transpose(fs[:, h, :], ot[:, T, h * P : (h + 1) * P], ident[:])
+            rs = stage.tile([P, 2, P], F32, name="rs", tag="rs", bufs=2)
+            nc.vector.tensor_copy(out=rs[:], in_=fs[:])
+            nc.sync.dma_start(out=out_1.rearrange("(h p) u -> p h u", p=P)[:, :, ucols], in_=rs[:])
+
+        for s in range(-3, n_units + 1):
+            if s + 3 < n_units:
+                load(s + 3)
+            if 0 <= s - 1:
+                turn(s - 1)
+                if (s - 1) % NG == NG - 1:
+                    gate_and_store((s - 1) // NG)
+            if 0 <= s < n_units:
+                quantize(s)
+            if 0 <= s + 2 < n_units:
+                widen(s + 2)
+            if 0 <= s < n_units:
+                experts(s)
+            if 0 <= s + 1 < n_units:
+                interleave(s + 1)
+            if s == 1:
+                build_gates()

@@ -42,9 +42,9 @@ def tile_plelayer_pa_kernel(
         x_sb = const.tile([P, 2, D], BF16, name="x_sb")
         nc.sync.dma_start(out=x_sb[:], in_=x.rearrange("(h p) d -> p h d", p=P))
         sc = const.tile([P, PACK], F32, name="sc")
-        nc.sync.dma_start(out=sc[:], in_=ew0_scale.rearrange("o (p j) a b -> p (o j a b)", j=PACK))
+        nc.scalar.dma_start(out=sc[:], in_=ew0_scale.rearrange("o (p j) a b -> p (o j a b)", j=PACK))
 
-        xt = psum.tile([P, 2, 2, P], F32, name="xt", tag="misc")
+        xt = psum.tile([P, 2, 2, P], F32, name="xt", tag="misc", bufs=1)
         for h in range(2):
             words = x_sb[:, h, :].bitcast(F32)
             for w in range(2):
@@ -60,8 +60,8 @@ def tile_plelayer_pa_kernel(
 
         bias_bf = const.tile([P, NG, UC, E], BF16, name="bias_bf")
         for t in range(T):
-            nc.gpsimd.dma_start(out=bias_bf[:, t, :, :], in_=eb0[t].rearrange("(c p) e -> p c e", p=P))
-        nc.gpsimd.dma_start(out=bias_bf[:, T, :, :], in_=ebs0.rearrange("(c p) e -> p c e", p=P))
+            nc.scalar.dma_start(out=bias_bf[:, t, :, :], in_=eb0[t].rearrange("(c p) e -> p c e", p=P))
+        nc.scalar.dma_start(out=bias_bf[:, T, :, :], in_=ebs0.rearrange("(c p) e -> p c e", p=P))
         bias_u = const.tile([P, NG, UC, E], F32, name="bias_u")
         nc.gpsimd.tensor_copy(out=bias_u[:], in_=bias_bf[:])
 
@@ -131,7 +131,7 @@ def tile_plelayer_pa_kernel(
                 nc.vector.tensor_tensor(out=fm[:, 6:NSLOT:2, :, :], in0=sh_t, in1=mask4, op=ALU.mult)
                 for s0 in range(0, NSLOT, 4):
                     n = min(4, NSLOT - s0)
-                    dps = psum.tile([P, 4, P], F32, name="dps", tag="misc")
+                    dps = psum.tile([P, 4, P], F32, name="dps", tag="misc", bufs=1)
                     for i in range(n):
                         nc.tensor.transpose(
                             dps[:, i, :], fm[:, s0 + i, :, :].rearrange("p e b -> p (e b)"), ident[:]
@@ -144,7 +144,7 @@ def tile_plelayer_pa_kernel(
         units = [(uc, g) for uc in range(UC) for g in GROUP_ORDER]
         n_units = len(units)
         raw, planes, grouped, codes, scales, relu_out = {}, {}, {}, {}, {}, {}
-        turned = {}
+        turned, sums, part = {}, {}, {}
 
         def load(i):
             uc, g = units[i]
@@ -158,39 +158,38 @@ def tile_plelayer_pa_kernel(
                 nc.sync.dma_start(out=wb[:], in_=ew0_bytes[g].rearrange("(p j) u e -> p j (u e)", j=PACK)[:, :, cols])
                 raw[i] = wb
 
-        def widen(i):
+        def widen(i, half):
             if units[i][1] == T:
                 return
-            wb = raw[i]
-            pl = stage.tile([P, PACK, SLAB], BF16, name="planes", tag="planes", bufs=3)
-            for j in range(PACK):
+            if half == 0:
+                planes[i] = stage.tile([P, PACK, SLAB], BF16, name="planes", tag="planes", bufs=3)
+            for j in (2 * half, 2 * half + 1):
                 nc.scalar.activation(
-                    out=pl[:, j, :], in_=wb[:, j, :].bitcast(FP8), func=ACT.Copy, scale=sc[:, j : j + 1]
+                    out=planes[i][:, j, :], in_=raw[i][:, j, :].bitcast(FP8), func=ACT.Copy, scale=sc[:, j : j + 1]
                 )
-            planes[i] = pl
 
-        def interleave(i):
-            pl = planes[i]
-            gr = stage.tile([P, PACK * SLAB], BF16, name="grp", tag="grp", bufs=2, align_bytes=64)
-            dst = gr[:].rearrange("p (e u j) -> p u e j", e=E, j=PACK)
-            src = pl[:].rearrange("p j (u e) -> p u e j", e=E)
-            for e0 in (0, 4):
-                nc.vector.tensor_copy(out=dst[:, :, e0 : e0 + 4, :], in_=src[:, :, e0 : e0 + 4, :])
-            grouped[i] = gr
+        def interleave(i, half):
+            if half == 0:
+                grouped[i] = stage.tile([P, PACK * SLAB], BF16, name="grp", tag="grp", bufs=2, align_bytes=64)
+            dst = grouped[i][:].rearrange("p (e u j) -> p u e j", e=E, j=PACK)
+            src = planes[i][:].rearrange("p j (u e) -> p u e j", e=E)
+            e0 = 4 * half
+            nc.vector.tensor_copy(out=dst[:, :, e0 : e0 + 4, :], in_=src[:, :, e0 : e0 + 4, :])
 
         def quantize(i):
-            gr = grouped[i]
             cd = stage.tile([P, SLAB], U32, name="wcodes", tag="wcodes", bufs=2, align_bytes=64)
             sl = stage.tile([P, SLAB], U8, name="wscl", tag="wscl", bufs=2, align_bytes=64)
-            nc.vector.quantize_mx(out=cd[:].bitcast(FP8X4), scales=sl[:], in_=gr[:])
+            nc.vector.quantize_mx(out=cd[:].bitcast(FP8X4), scales=sl[:], in_=grouped[i][:])
             codes[i], scales[i] = cd, sl
 
-        def experts(i):
+        def experts(i, half):
             uc, g = units[i]
             cd, sl = codes[i], scales[i]
-            hs = stage.tile([P, BC, E, NB], F32, name="hs", tag="hs", bufs=2)
-            for e0 in range(0, E, 2):
-                z = psum.tile([P, 2, B], F32, name="z", tag="z")
+            if half == 0:
+                relu_out[i] = stage.tile([P, BC, E, NB], F32, name="hs", tag="hs", bufs=2)
+            hs = relu_out[i]
+            for e0 in (4 * half, 4 * half + 2):
+                z = psum.tile([P, 2, B], F32, name="z", tag="z", bufs=3)
                 for k in range(2):
                     cols = slice((e0 + k) * P, (e0 + k + 1) * P)
                     nc.tensor.matmul_mx(
@@ -211,73 +210,103 @@ def tile_plelayer_pa_kernel(
                         bias=bias_u[:, g, uc, e : e + 1],
                         scale=1.0,
                     )
-            relu_out[i] = hs
 
-        def turn(i):
+        def turn(i, q):
+            if q == 0:
+                turned[i] = stage.tile([P, BC, P], F32, name="ht", tag="ht", bufs=3)
+            hs, ht = relu_out[i], turned[i]
+            tp = psum.tile([P, 4, P], F32, name="tp", tag="tp", bufs=2)
+            for k in range(4):
+                nc.tensor.transpose(tp[:, k, :], hs[:, 4 * q + k, :, :].rearrange("p e b -> p (e b)"), ident[:])
+            nc.vector.tensor_copy(out=ht[:, 4 * q : 4 * q + 4, :], in_=tp[:])
+
+        def gate(i, half):
             uc, g = units[i]
-            hs = relu_out[i]
-            ht = stage.tile([P, BC, P], F32, name="ht%d" % g, tag="ht%d" % g, bufs=2)
-            for q in range(4):
-                tp = psum.tile([P, 4, P], F32, name="tp", tag="tp")
-                for k in range(4):
-                    nc.tensor.transpose(tp[:, k, :], hs[:, 4 * q + k, :, :].rearrange("p e b -> p (e b)"), ident[:])
-                nc.vector.tensor_copy(out=ht[:, 4 * q : 4 * q + 4, :], in_=tp[:])
-            turned[g] = ht
-
-        def gate_and_store(uc):
-            ot = stage.tile([P, NG, B], F32, name="ot", tag="ot", bufs=2)
-            for q in range(4):
-                o = psum.tile([P, 4, NG, NB], F32, name="o", tag="o")
-                for k in range(4):
-                    bc = 4 * q + k
-                    nc.tensor.matmul(
-                        out=o[:, k, :, :].rearrange("p j b -> p (j b)"),
-                        lhsT=turned[T][:, bc, :],
-                        rhs=dall[:, bc, 0:NG, :].rearrange("p s b -> p (s b)"),
-                        start=True,
-                        stop=False,
-                    )
-                    for t in range(T):
+            ht = turned[i]
+            if g == T:
+                if half == 0:
+                    sums[uc] = stage.tile([P, NG, B], F32, name="ot", tag="ot", bufs=2)
+                ot = sums[uc]
+                for q in (2 * half, 2 * half + 1):
+                    o = psum.tile([P, 4, NG, NB], F32, name="o", tag="o", bufs=2)
+                    for k in range(4):
+                        bc = 4 * q + k
                         nc.tensor.matmul(
-                            out=o[:, k, t : NG : T - t, :],
-                            lhsT=turned[t][:, bc, :],
-                            rhs=dall[:, bc, 5 + 2 * t : 7 + 2 * t, :],
-                            start=False,
-                            stop=(t == T - 1),
+                            out=o[:, k, :, :].rearrange("p j b -> p (j b)"),
+                            lhsT=ht[:, bc, :],
+                            rhs=dall[:, bc, 0:NG, :].rearrange("p s b -> p (s b)"),
+                            start=True,
+                            stop=True,
                         )
-                nc.vector.tensor_copy(
-                    out=ot[:, :, 64 * q : 64 * q + 64].rearrange("p j (k b) -> p k j b", b=NB), in_=o[:]
-                )
+                    nc.vector.tensor_copy(
+                        out=ot[:, :, 64 * q : 64 * q + 64].rearrange("p j (k b) -> p k j b", b=NB), in_=o[:]
+                    )
+            else:
+                if half == 0:
+                    part[i] = psum.tile([P, BC, 2, NB], F32, name="o", tag="o", bufs=2)
+                o = part[i]
+                for bc in range(8 * half, 8 * half + 8):
+                    nc.tensor.matmul(
+                        out=o[:, bc, :, :].rearrange("p s b -> p (s b)"),
+                        lhsT=ht[:, bc, :],
+                        rhs=dall[:, bc, 5 + 2 * g : 7 + 2 * g, :].rearrange("p s b -> p (s b)"),
+                        start=True,
+                        stop=True,
+                    )
+                if half == 1:
+                    both = sums[uc][:, g : NG : T - g, :].rearrange("p s (c b) -> p s c b", b=NB)
+                    nc.vector.tensor_tensor(out=both, in0=o[:].rearrange("p c s b -> p s c b"), in1=both, op=ALU.add)
+
+        def store(uc):
+            ot = sums[uc]
             ucols = slice(uc * P, (uc + 1) * P)
             for h in range(2):
                 rows = slice(h * P, (h + 1) * P)
-                fp = psum.tile([P, T, P], F32, name="fp", tag="misc")
+                fp = psum.tile([P, T, P], F32, name="fp", tag="misc", bufs=1)
                 for t in range(T):
                     nc.tensor.transpose(fp[:, t, :], ot[:, t, rows], ident[:])
                 res = stage.tile([P, T, P], F32, name="res", tag="res", bufs=2)
                 nc.vector.tensor_copy(out=res[:], in_=fp[:])
                 nc.sync.dma_start(out=out_0[:, rows, ucols].rearrange("t p u -> p t u"), in_=res[:])
-            fs = psum.tile([P, 2, P], F32, name="fs", tag="misc")
+            fs = psum.tile([P, 2, P], F32, name="fs", tag="misc", bufs=1)
             for h in range(2):
                 nc.tensor.transpose(fs[:, h, :], ot[:, T, h * P : (h + 1) * P], ident[:])
             rs = stage.tile([P, 2, P], F32, name="rs", tag="rs", bufs=2)
             nc.vector.tensor_copy(out=rs[:], in_=fs[:])
             nc.sync.dma_start(out=out_1.rearrange("(h p) u -> p h u", p=P)[:, :, ucols], in_=rs[:])
 
-        for s in range(-3, n_units + 1):
-            if s + 3 < n_units:
+        def live(i):
+            return 0 <= i < n_units
+
+        for s in range(-3, n_units + 2):
+            if live(s + 3):
                 load(s + 3)
-            if 0 <= s - 1:
-                turn(s - 1)
-                if (s - 1) % NG == NG - 1:
-                    gate_and_store((s - 1) // NG)
-            if 0 <= s < n_units:
+            if live(s - 1):
+                turn(s - 1, 0)
+            if live(s):
                 quantize(s)
-            if 0 <= s + 2 < n_units:
-                widen(s + 2)
-            if 0 <= s < n_units:
-                experts(s)
-            if 0 <= s + 1 < n_units:
-                interleave(s + 1)
-            if s == 1:
+            if live(s - 1):
+                turn(s - 1, 1)
+            if live(s + 2):
+                widen(s + 2, 0)
+            if live(s - 2):
+                gate(s - 2, 0)
+            if live(s):
+                experts(s, 0)
+            if live(s + 1):
+                interleave(s + 1, 0)
+            if live(s - 1):
+                turn(s - 1, 2)
+                turn(s - 1, 3)
+            if live(s + 2):
+                widen(s + 2, 1)
+            if live(s - 2):
+                gate(s - 2, 1)
+            if live(s):
+                experts(s, 1)
+            if live(s + 1):
+                interleave(s + 1, 1)
+            if live(s - 2) and (s - 2) % NG == NG - 1:
+                store((s - 2) // NG)
+            if s == 0:
                 build_gates()

@@ -25,6 +25,7 @@ BC = B // NB
 SLAB = P * E
 NSLOT = 13
 GROUP_ORDER = (T, 0, 1, 2, 3)
+WARM = True
 
 
 def tile_plelayer_pa_kernel(
@@ -67,18 +68,19 @@ def tile_plelayer_pa_kernel(
 
         lg_t = const.tile([P, 2, 64], BF16, name="lg_t")
         for h in range(2):
-            nc.gpsimd.dma_start(
+            nc.scalar.dma_start(
                 out=lg_t[:, h, :].rearrange("p (t k) -> p t k", t=T),
                 in_=gate_pre0[:, h * P : (h + 1) * P, :].rearrange("t p k -> p t k"),
             )
         lg_s = const.tile([P, 2, 40], BF16, name="lg_s")
-        nc.gpsimd.dma_start(out=lg_s[:], in_=sgate_pre.rearrange("(h p) k -> p h k", p=P))
+        nc.scalar.dma_start(out=lg_s[:], in_=sgate_pre.rearrange("(h p) k -> p h k", p=P))
         gb_t = const.tile([P, 64], BF16, name="gb_t")
-        nc.gpsimd.dma_start(out=gb_t[:], in_=gb0.rearrange("t k -> (t k)").partition_broadcast(P))
+        nc.scalar.dma_start(out=gb_t[:], in_=gb0.rearrange("t k -> (t k)").partition_broadcast(P))
         gb_s = const.tile([P, 40], BF16, name="gb_s")
-        nc.gpsimd.dma_start(out=gb_s[:], in_=gbs.partition_broadcast(P))
+        nc.scalar.dma_start(out=gb_s[:], in_=gbs.partition_broadcast(P))
 
         dall = const.tile([P, BC, NSLOT, NB], F32, name="dall")
+        spread = {}
 
         def build_gates():
             gl = const.tile([P, 2, 104], F32, name="gl")
@@ -118,6 +120,7 @@ def tile_plelayer_pa_kernel(
             mask4 = mask[:].unsqueeze(1).unsqueeze(1).to_broadcast([P, T, E, NB])
             for h in range(2):
                 fm = const.tile([P, NSLOT, E, NB], F32, name="fm", tag="fm", bufs=2)
+                spread[h] = fm
                 halves = gl[:, h, 0:64].rearrange("p (t s e) -> p t s e", t=T, s=2)
                 own = halves[:, :, 0, :].unsqueeze(3).to_broadcast([P, T, E, NB])
                 shared = halves[:, :, 1, :].unsqueeze(3).to_broadcast([P, T, E, NB])
@@ -129,17 +132,18 @@ def tile_plelayer_pa_kernel(
                 )
                 nc.vector.tensor_tensor(out=fm[:, 5:NSLOT:2, :, :], in0=own, in1=mask4, op=ALU.mult)
                 nc.vector.tensor_tensor(out=fm[:, 6:NSLOT:2, :, :], in0=sh_t, in1=mask4, op=ALU.mult)
-                for s0 in range(0, NSLOT, 4):
-                    n = min(4, NSLOT - s0)
-                    dps = psum.tile([P, 4, P], F32, name="dps", tag="misc", bufs=1)
-                    for i in range(n):
-                        nc.tensor.transpose(
-                            dps[:, i, :], fm[:, s0 + i, :, :].rearrange("p e b -> p (e b)"), ident[:]
-                        )
-                    nc.vector.tensor_copy(
-                        out=dall[:, 8 * h : 8 * h + 8, s0 : s0 + n, :].rearrange("p c s b -> p s c b"),
-                        in_=dps[:, 0:n, :].rearrange("p s (c b) -> p s c b", b=NB),
-                    )
+
+        def turn_gates(h, s0):
+            n = min(4, NSLOT - s0)
+            dps = psum.tile([P, 4, P], F32, name="dps", tag="misc", bufs=1)
+            for i in range(n):
+                nc.tensor.transpose(
+                    dps[:, i, :], spread[h][:, s0 + i, :, :].rearrange("p e b -> p (e b)"), ident[:]
+                )
+            nc.vector.tensor_copy(
+                out=dall[:, 8 * h : 8 * h + 8, s0 : s0 + n, :].rearrange("p c s b -> p s c b"),
+                in_=dps[:, 0:n, :].rearrange("p s (c b) -> p s c b", b=NB),
+            )
 
         units = [(uc, g) for uc in range(UC) for g in GROUP_ORDER]
         n_units = len(units)
@@ -158,15 +162,14 @@ def tile_plelayer_pa_kernel(
                 nc.sync.dma_start(out=wb[:], in_=ew0_bytes[g].rearrange("(p j) u e -> p j (u e)", j=PACK)[:, :, cols])
                 raw[i] = wb
 
-        def widen(i, half):
+        def widen(i, j):
             if units[i][1] == T:
                 return
-            if half == 0:
+            if j == 0:
                 planes[i] = stage.tile([P, PACK, SLAB], BF16, name="planes", tag="planes", bufs=3)
-            for j in (2 * half, 2 * half + 1):
-                nc.scalar.activation(
-                    out=planes[i][:, j, :], in_=raw[i][:, j, :].bitcast(FP8), func=ACT.Copy, scale=sc[:, j : j + 1]
-                )
+            nc.scalar.activation(
+                out=planes[i][:, j, :], in_=raw[i][:, j, :].bitcast(FP8), func=ACT.Copy, scale=sc[:, j : j + 1]
+            )
 
         def interleave(i, half):
             if half == 0:
@@ -177,39 +180,49 @@ def tile_plelayer_pa_kernel(
             nc.vector.tensor_copy(out=dst[:, :, e0 : e0 + 4, :], in_=src[:, :, e0 : e0 + 4, :])
 
         def quantize(i):
-            cd = stage.tile([P, SLAB], U32, name="wcodes", tag="wcodes", bufs=2, align_bytes=64)
-            sl = stage.tile([P, SLAB], U8, name="wscl", tag="wscl", bufs=2, align_bytes=64)
+            cd = stage.tile([P, SLAB], U32, name="wcodes", tag="wcodes", bufs=3, align_bytes=64)
+            sl = stage.tile([P, SLAB], U8, name="wscl", tag="wscl", bufs=3, align_bytes=64)
             nc.vector.quantize_mx(out=cd[:].bitcast(FP8X4), scales=sl[:], in_=grouped[i][:])
             codes[i], scales[i] = cd, sl
 
-        def experts(i, half):
+        def experts(i, q):
             uc, g = units[i]
             cd, sl = codes[i], scales[i]
-            if half == 0:
+            if q == 0:
                 relu_out[i] = stage.tile([P, BC, E, NB], F32, name="hs", tag="hs", bufs=2)
             hs = relu_out[i]
-            for e0 in (4 * half, 4 * half + 2):
-                z = psum.tile([P, 2, B], F32, name="z", tag="z", bufs=3)
-                for k in range(2):
-                    cols = slice((e0 + k) * P, (e0 + k + 1) * P)
-                    nc.tensor.matmul_mx(
-                        out=z[:, k, :],
-                        lhsT=cd[:, cols].bitcast(FP8X4),
-                        lhsT_scale=sl[:, cols],
-                        rhs=xcodes[:].bitcast(FP8X4),
-                        rhs_scale=xscl[:],
-                        start=True,
-                        stop=True,
-                    )
-                for k in range(2):
-                    e = e0 + k
-                    nc.scalar.activation(
-                        out=hs[:, :, e, :],
-                        in_=z[:, k, :].rearrange("p (c b) -> p c b", b=NB),
-                        func=ACT.Relu,
-                        bias=bias_u[:, g, uc, e : e + 1],
-                        scale=1.0,
-                    )
+            e0 = 2 * q
+            z = psum.tile([P, 2, B], F32, name="z", tag="z", bufs=3)
+            if WARM:
+                nc.tensor.matmul_mx(
+                    out=z[:].rearrange("p k b -> p (k b)"),
+                    lhsT=cd[:, e0 * P : (e0 + 1) * P].bitcast(FP8X4),
+                    lhsT_scale=sl[:, e0 * P : (e0 + 1) * P],
+                    rhs=cd[:, 0 : 2 * B].bitcast(FP8X4),
+                    rhs_scale=sl[:, 0 : 2 * B],
+                    start=True,
+                    stop=True,
+                )
+            for k in range(2):
+                cols = slice((e0 + k) * P, (e0 + k + 1) * P)
+                nc.tensor.matmul_mx(
+                    out=z[:, k, :],
+                    lhsT=cd[:, cols].bitcast(FP8X4),
+                    lhsT_scale=sl[:, cols],
+                    rhs=xcodes[:].bitcast(FP8X4),
+                    rhs_scale=xscl[:],
+                    start=True,
+                    stop=True,
+                )
+            for k in range(2):
+                e = e0 + k
+                nc.scalar.activation(
+                    out=hs[:, :, e, :],
+                    in_=z[:, k, :].rearrange("p (c b) -> p c b", b=NB),
+                    func=ACT.Relu,
+                    bias=bias_u[:, g, uc, e : e + 1],
+                    scale=1.0,
+                )
 
         def turn(i, q):
             if q == 0:
@@ -220,32 +233,30 @@ def tile_plelayer_pa_kernel(
                 nc.tensor.transpose(tp[:, k, :], hs[:, 4 * q + k, :, :].rearrange("p e b -> p (e b)"), ident[:])
             nc.vector.tensor_copy(out=ht[:, 4 * q : 4 * q + 4, :], in_=tp[:])
 
-        def gate(i, half):
+        def gate(i, q):
             uc, g = units[i]
             ht = turned[i]
             if g == T:
-                if half == 0:
+                if q == 0:
                     sums[uc] = stage.tile([P, NG, B], F32, name="ot", tag="ot", bufs=2)
-                ot = sums[uc]
-                for q in (2 * half, 2 * half + 1):
-                    o = psum.tile([P, 4, NG, NB], F32, name="o", tag="o", bufs=2)
-                    for k in range(4):
-                        bc = 4 * q + k
-                        nc.tensor.matmul(
-                            out=o[:, k, :, :].rearrange("p j b -> p (j b)"),
-                            lhsT=ht[:, bc, :],
-                            rhs=dall[:, bc, 0:NG, :].rearrange("p s b -> p (s b)"),
-                            start=True,
-                            stop=True,
-                        )
-                    nc.vector.tensor_copy(
-                        out=ot[:, :, 64 * q : 64 * q + 64].rearrange("p j (k b) -> p k j b", b=NB), in_=o[:]
+                o = psum.tile([P, 4, NG, NB], F32, name="o", tag="o", bufs=2)
+                for k in range(4):
+                    bc = 4 * q + k
+                    nc.tensor.matmul(
+                        out=o[:, k, :, :].rearrange("p j b -> p (j b)"),
+                        lhsT=ht[:, bc, :],
+                        rhs=dall[:, bc, 0:NG, :].rearrange("p s b -> p (s b)"),
+                        start=True,
+                        stop=True,
                     )
+                nc.vector.tensor_copy(
+                    out=sums[uc][:, :, 64 * q : 64 * q + 64].rearrange("p j (k b) -> p k j b", b=NB), in_=o[:]
+                )
             else:
-                if half == 0:
+                if q == 0:
                     part[i] = psum.tile([P, BC, 2, NB], F32, name="o", tag="o", bufs=2)
                 o = part[i]
-                for bc in range(8 * half, 8 * half + 8):
+                for bc in range(4 * q, 4 * q + 4):
                     nc.tensor.matmul(
                         out=o[:, bc, :, :].rearrange("p s b -> p (s b)"),
                         lhsT=ht[:, bc, :],
@@ -253,60 +264,59 @@ def tile_plelayer_pa_kernel(
                         start=True,
                         stop=True,
                     )
-                if half == 1:
-                    both = sums[uc][:, g : NG : T - g, :].rearrange("p s (c b) -> p s c b", b=NB)
-                    nc.vector.tensor_tensor(out=both, in0=o[:].rearrange("p c s b -> p s c b"), in1=both, op=ALU.add)
 
-        def store(uc):
+        def add_up(i):
+            uc, g = units[i]
+            if g != T:
+                both = sums[uc][:, g : NG : T - g, :].rearrange("p s (c b) -> p s c b", b=NB)
+                nc.vector.tensor_tensor(
+                    out=both, in0=part[i][:].rearrange("p c s b -> p s c b"), in1=both, op=ALU.add
+                )
+
+        def store(uc, k):
             ot = sums[uc]
             ucols = slice(uc * P, (uc + 1) * P)
-            for h in range(2):
-                rows = slice(h * P, (h + 1) * P)
+            if k < 2:
+                rows = slice(k * P, (k + 1) * P)
                 fp = psum.tile([P, T, P], F32, name="fp", tag="misc", bufs=1)
                 for t in range(T):
                     nc.tensor.transpose(fp[:, t, :], ot[:, t, rows], ident[:])
                 res = stage.tile([P, T, P], F32, name="res", tag="res", bufs=2)
                 nc.vector.tensor_copy(out=res[:], in_=fp[:])
                 nc.sync.dma_start(out=out_0[:, rows, ucols].rearrange("t p u -> p t u"), in_=res[:])
-            fs = psum.tile([P, 2, P], F32, name="fs", tag="misc", bufs=1)
-            for h in range(2):
-                nc.tensor.transpose(fs[:, h, :], ot[:, T, h * P : (h + 1) * P], ident[:])
-            rs = stage.tile([P, 2, P], F32, name="rs", tag="rs", bufs=2)
-            nc.vector.tensor_copy(out=rs[:], in_=fs[:])
-            nc.sync.dma_start(out=out_1.rearrange("(h p) u -> p h u", p=P)[:, :, ucols], in_=rs[:])
+            else:
+                fs = psum.tile([P, 2, P], F32, name="fs", tag="misc", bufs=1)
+                for h in range(2):
+                    nc.tensor.transpose(fs[:, h, :], ot[:, T, h * P : (h + 1) * P], ident[:])
+                rs = stage.tile([P, 2, P], F32, name="rs", tag="rs", bufs=2)
+                nc.vector.tensor_copy(out=rs[:], in_=fs[:])
+                nc.sync.dma_start(out=out_1.rearrange("(h p) u -> p h u", p=P)[:, :, ucols], in_=rs[:])
 
         def live(i):
             return 0 <= i < n_units
 
-        for s in range(-3, n_units + 2):
-            if live(s + 3):
-                load(s + 3)
-            if live(s - 1):
-                turn(s - 1, 0)
-            if live(s):
-                quantize(s)
-            if live(s - 1):
-                turn(s - 1, 1)
-            if live(s + 2):
-                widen(s + 2, 0)
-            if live(s - 2):
-                gate(s - 2, 0)
-            if live(s):
-                experts(s, 0)
-            if live(s + 1):
-                interleave(s + 1, 0)
-            if live(s - 1):
-                turn(s - 1, 2)
-                turn(s - 1, 3)
-            if live(s + 2):
-                widen(s + 2, 1)
-            if live(s - 2):
-                gate(s - 2, 1)
-            if live(s):
-                experts(s, 1)
-            if live(s + 1):
-                interleave(s + 1, 1)
-            if live(s - 2) and (s - 2) % NG == NG - 1:
-                store((s - 2) // NG)
-            if s == 0:
-                build_gates()
+        with tc.manual_schedule(engines={mybir.EngineType.PE}):
+            for s in range(-4, n_units + 4):
+                if live(s + 4):
+                    load(s + 4)
+                if live(s - 3):
+                    add_up(s - 3)
+                for q in range(4):
+                    if live(s + 3):
+                        widen(s + 3, q)
+                    if live(s + 2) and q % 2 == 0:
+                        interleave(s + 2, q // 2)
+                    if live(s):
+                        experts(s, q)
+                    if live(s - 2):
+                        gate(s - 2, q)
+                    if live(s - 1):
+                        turn(s - 1, q)
+                    if live(s + 1) and q == 1:
+                        quantize(s + 1)
+                    if s in (0, 1):
+                        turn_gates(s, 4 * q)
+                    if live(s - 3) and (s - 3) % NG == NG - 1 and q < 3:
+                        store((s - 3) // NG, q)
+                if s == -1:
+                    build_gates()

@@ -25,7 +25,8 @@ BC = B // NB
 SLAB = P * E
 NSLOT = 13
 GROUP_ORDER = (T, 0, 1, 2, 3)
-WARM = True
+WARM = (0, 1, 2, 3)
+TURN_ON_SCALAR = (3,)
 
 
 def tile_plelayer_pa_kernel(
@@ -148,7 +149,7 @@ def tile_plelayer_pa_kernel(
         units = [(uc, g) for uc in range(UC) for g in GROUP_ORDER]
         n_units = len(units)
         raw, planes, grouped, codes, scales, relu_out = {}, {}, {}, {}, {}, {}
-        turned, sums, part = {}, {}, {}
+        turned, sums, part, banks = {}, {}, {}, {}
 
         def load(i):
             uc, g = units[i]
@@ -185,40 +186,39 @@ def tile_plelayer_pa_kernel(
             nc.vector.quantize_mx(out=cd[:].bitcast(FP8X4), scales=sl[:], in_=grouped[i][:])
             codes[i], scales[i] = cd, sl
 
-        def experts(i, q):
-            uc, g = units[i]
+        def mx_pass(out, cd, sl, e, rhs, rhs_scale):
+            cols = slice(e * P, (e + 1) * P)
+            nc.tensor.matmul_mx(
+                out=out,
+                lhsT=cd[:, cols].bitcast(FP8X4),
+                lhsT_scale=sl[:, cols],
+                rhs=rhs.bitcast(FP8X4),
+                rhs_scale=rhs_scale,
+                start=True,
+                stop=True,
+            )
+
+        def expert_passes(i, q):
             cd, sl = codes[i], scales[i]
             if q == 0:
                 relu_out[i] = stage.tile([P, BC, E, NB], F32, name="hs", tag="hs", bufs=2)
-            hs = relu_out[i]
             e0 = 2 * q
             z = psum.tile([P, 2, B], F32, name="z", tag="z", bufs=3)
-            if WARM:
-                nc.tensor.matmul_mx(
-                    out=z[:].rearrange("p k b -> p (k b)"),
-                    lhsT=cd[:, e0 * P : (e0 + 1) * P].bitcast(FP8X4),
-                    lhsT_scale=sl[:, e0 * P : (e0 + 1) * P],
-                    rhs=cd[:, 0 : 2 * B].bitcast(FP8X4),
-                    rhs_scale=sl[:, 0 : 2 * B],
-                    start=True,
-                    stop=True,
-                )
+            banks[i] = z
+            ops = []
+            if q in WARM:
+                ops.append(lambda: mx_pass(z[:, 0, :], cd, sl, e0, xcodes[:], xscl[:]))
+            ops.append(lambda: mx_pass(z[:, 0, :], cd, sl, e0, xcodes[:], xscl[:]))
+            ops.append(lambda: mx_pass(z[:, 1, :], cd, sl, e0 + 1, xcodes[:], xscl[:]))
+            return ops
+
+        def expert_relu(i, q):
+            uc, g = units[i]
             for k in range(2):
-                cols = slice((e0 + k) * P, (e0 + k + 1) * P)
-                nc.tensor.matmul_mx(
-                    out=z[:, k, :],
-                    lhsT=cd[:, cols].bitcast(FP8X4),
-                    lhsT_scale=sl[:, cols],
-                    rhs=xcodes[:].bitcast(FP8X4),
-                    rhs_scale=xscl[:],
-                    start=True,
-                    stop=True,
-                )
-            for k in range(2):
-                e = e0 + k
+                e = 2 * q + k
                 nc.scalar.activation(
-                    out=hs[:, :, e, :],
-                    in_=z[:, k, :].rearrange("p (c b) -> p c b", b=NB),
+                    out=relu_out[i][:, :, e, :],
+                    in_=banks[i][:, k, :].rearrange("p (c b) -> p c b", b=NB),
                     func=ACT.Relu,
                     bias=bias_u[:, g, uc, e : e + 1],
                     scale=1.0,
@@ -231,39 +231,40 @@ def tile_plelayer_pa_kernel(
             tp = psum.tile([P, 4, P], F32, name="tp", tag="tp", bufs=2)
             for k in range(4):
                 nc.tensor.transpose(tp[:, k, :], hs[:, 4 * q + k, :, :].rearrange("p e b -> p (e b)"), ident[:])
-            nc.vector.tensor_copy(out=ht[:, 4 * q : 4 * q + 4, :], in_=tp[:])
+            if q in TURN_ON_SCALAR:
+                nc.scalar.copy(out=ht[:, 4 * q : 4 * q + 4, :], in_=tp[:])
+            else:
+                nc.vector.tensor_copy(out=ht[:, 4 * q : 4 * q + 4, :], in_=tp[:])
 
-        def gate(i, q):
+        def gate_pass(out, ht, bc, s0, s1):
+            nc.tensor.matmul(
+                out=out.rearrange("p s b -> p (s b)"),
+                lhsT=ht[:, bc, :],
+                rhs=dall[:, bc, s0:s1, :].rearrange("p s b -> p (s b)"),
+                start=True,
+                stop=True,
+            )
+
+        def gate_passes(i, q):
             uc, g = units[i]
             ht = turned[i]
             if g == T:
                 if q == 0:
                     sums[uc] = stage.tile([P, NG, B], F32, name="ot", tag="ot", bufs=2)
                 o = psum.tile([P, 4, NG, NB], F32, name="o", tag="o", bufs=2)
-                for k in range(4):
-                    bc = 4 * q + k
-                    nc.tensor.matmul(
-                        out=o[:, k, :, :].rearrange("p j b -> p (j b)"),
-                        lhsT=ht[:, bc, :],
-                        rhs=dall[:, bc, 0:NG, :].rearrange("p s b -> p (s b)"),
-                        start=True,
-                        stop=True,
-                    )
+                part[i] = o
+                return [lambda k=k: gate_pass(o[:, k, :, :], ht, 4 * q + k, 0, NG) for k in range(4)]
+            if q == 0:
+                part[i] = psum.tile([P, BC, 2, NB], F32, name="o", tag="o", bufs=2)
+            o = part[i]
+            return [lambda k=k: gate_pass(o[:, 4 * q + k, :, :], ht, 4 * q + k, 5 + 2 * g, 7 + 2 * g) for k in range(4)]
+
+        def gate_copy(i, q):
+            uc, g = units[i]
+            if g == T:
                 nc.vector.tensor_copy(
-                    out=sums[uc][:, :, 64 * q : 64 * q + 64].rearrange("p j (k b) -> p k j b", b=NB), in_=o[:]
+                    out=sums[uc][:, :, 64 * q : 64 * q + 64].rearrange("p j (k b) -> p k j b", b=NB), in_=part[i][:]
                 )
-            else:
-                if q == 0:
-                    part[i] = psum.tile([P, BC, 2, NB], F32, name="o", tag="o", bufs=2)
-                o = part[i]
-                for bc in range(4 * q, 4 * q + 4):
-                    nc.tensor.matmul(
-                        out=o[:, bc, :, :].rearrange("p s b -> p (s b)"),
-                        lhsT=ht[:, bc, :],
-                        rhs=dall[:, bc, 5 + 2 * g : 7 + 2 * g, :].rearrange("p s b -> p (s b)"),
-                        start=True,
-                        stop=True,
-                    )
 
         def add_up(i):
             uc, g = units[i]
@@ -282,14 +283,14 @@ def tile_plelayer_pa_kernel(
                 for t in range(T):
                     nc.tensor.transpose(fp[:, t, :], ot[:, t, rows], ident[:])
                 res = stage.tile([P, T, P], F32, name="res", tag="res", bufs=2)
-                nc.vector.tensor_copy(out=res[:], in_=fp[:])
+                nc.scalar.copy(out=res[:], in_=fp[:])
                 nc.sync.dma_start(out=out_0[:, rows, ucols].rearrange("t p u -> p t u"), in_=res[:])
             else:
                 fs = psum.tile([P, 2, P], F32, name="fs", tag="misc", bufs=1)
                 for h in range(2):
                     nc.tensor.transpose(fs[:, h, :], ot[:, T, h * P : (h + 1) * P], ident[:])
                 rs = stage.tile([P, 2, P], F32, name="rs", tag="rs", bufs=2)
-                nc.vector.tensor_copy(out=rs[:], in_=fs[:])
+                nc.scalar.copy(out=rs[:], in_=fs[:])
                 nc.sync.dma_start(out=out_1.rearrange("(h p) u -> p h u", p=P)[:, :, ucols], in_=rs[:])
 
         def live(i):
@@ -306,10 +307,17 @@ def tile_plelayer_pa_kernel(
                         widen(s + 3, q)
                     if live(s + 2) and q % 2 == 0:
                         interleave(s + 2, q // 2)
+                    wide = expert_passes(s, q) if live(s) else []
+                    thin = gate_passes(s - 2, q) if live(s - 2) else []
+                    for n in range(4):
+                        if n < len(thin):
+                            thin[n]()
+                        if n < len(wide):
+                            wide[n]()
                     if live(s):
-                        experts(s, q)
+                        expert_relu(s, q)
                     if live(s - 2):
-                        gate(s - 2, q)
+                        gate_copy(s - 2, q)
                     if live(s - 1):
                         turn(s - 1, q)
                     if live(s + 1) and q == 1:

@@ -26,7 +26,8 @@ SLAB = P * E
 NSLOT = 13
 GROUP_ORDER = (T, 0, 1, 2, 3)
 WARM = (0, 1, 2, 3)
-TURN_ON_SCALAR = (3,)
+TURN_ON_SCALAR = (1, 2, 3)
+WIDEN_ON_VECTOR = (1, 3)
 
 
 def tile_plelayer_pa_kernel(
@@ -38,13 +39,16 @@ def tile_plelayer_pa_kernel(
         stage = ctx.enter_context(tc.tile_pool(name="stage", bufs=2))
         psum = ctx.enter_context(tc.psum_pool(name="psum", bufs=2))
 
+        warm = const.tile([P, 1], F32, name="warm")
+        nc.vector.memset(warm[:], 0.0)
+        nc.scalar.activation(out=warm[:], in_=warm[:], func=ACT.Exp)
+
         ident = const.tile([P, P], F32, name="ident")
         make_identity(nc, ident[:])
 
         x_sb = const.tile([P, 2, D], BF16, name="x_sb")
         nc.sync.dma_start(out=x_sb[:], in_=x.rearrange("(h p) d -> p h d", p=P))
         sc = const.tile([P, PACK], F32, name="sc")
-        nc.scalar.dma_start(out=sc[:], in_=ew0_scale.rearrange("o (p j) a b -> p (o j a b)", j=PACK))
 
         xt = psum.tile([P, 2, 2, P], F32, name="xt", tag="misc", bufs=1)
         for h in range(2):
@@ -61,24 +65,31 @@ def tile_plelayer_pa_kernel(
         nc.vector.quantize_mx(out=xcodes[:].bitcast(FP8X4), scales=xscl[:], in_=xg[:])
 
         bias_bf = const.tile([P, NG, UC, E], BF16, name="bias_bf")
-        for t in range(T):
-            nc.scalar.dma_start(out=bias_bf[:, t, :, :], in_=eb0[t].rearrange("(c p) e -> p c e", p=P))
-        nc.scalar.dma_start(out=bias_bf[:, T, :, :], in_=ebs0.rearrange("(c p) e -> p c e", p=P))
         bias_u = const.tile([P, NG, UC, E], F32, name="bias_u")
-        nc.gpsimd.tensor_copy(out=bias_u[:], in_=bias_bf[:])
+
+        def load_scale():
+            nc.sync.dma_start(out=sc[:], in_=ew0_scale.rearrange("o (p j) a b -> p (o j a b)", j=PACK))
+
+        def load_biases():
+            nc.sync.dma_start(out=bias_bf[:, T, :, :], in_=ebs0.rearrange("(c p) e -> p c e", p=P))
+            for t in range(T):
+                nc.sync.dma_start(out=bias_bf[:, t, :, :], in_=eb0[t].rearrange("(c p) e -> p c e", p=P))
+            nc.gpsimd.tensor_copy(out=bias_u[:], in_=bias_bf[:])
 
         lg_t = const.tile([P, 2, 64], BF16, name="lg_t")
-        for h in range(2):
-            nc.scalar.dma_start(
-                out=lg_t[:, h, :].rearrange("p (t k) -> p t k", t=T),
-                in_=gate_pre0[:, h * P : (h + 1) * P, :].rearrange("t p k -> p t k"),
-            )
         lg_s = const.tile([P, 2, 40], BF16, name="lg_s")
-        nc.scalar.dma_start(out=lg_s[:], in_=sgate_pre.rearrange("(h p) k -> p h k", p=P))
         gb_t = const.tile([P, 64], BF16, name="gb_t")
-        nc.scalar.dma_start(out=gb_t[:], in_=gb0.rearrange("t k -> (t k)").partition_broadcast(P))
         gb_s = const.tile([P, 40], BF16, name="gb_s")
-        nc.scalar.dma_start(out=gb_s[:], in_=gbs.partition_broadcast(P))
+
+        def load_gates():
+            for h in range(2):
+                nc.sync.dma_start(
+                    out=lg_t[:, h, :].rearrange("p (t k) -> p t k", t=T),
+                    in_=gate_pre0[:, h * P : (h + 1) * P, :].rearrange("t p k -> p t k"),
+                )
+            nc.sync.dma_start(out=lg_s[:], in_=sgate_pre.rearrange("(h p) k -> p h k", p=P))
+            nc.sync.dma_start(out=gb_t[:], in_=gb0.rearrange("t k -> (t k)").partition_broadcast(P))
+            nc.sync.dma_start(out=gb_s[:], in_=gbs.partition_broadcast(P))
 
         dall = const.tile([P, BC, NSLOT, NB], F32, name="dall")
         spread = {}
@@ -168,9 +179,18 @@ def tile_plelayer_pa_kernel(
                 return
             if j == 0:
                 planes[i] = stage.tile([P, PACK, SLAB], BF16, name="planes", tag="planes", bufs=3)
-            nc.scalar.activation(
-                out=planes[i][:, j, :], in_=raw[i][:, j, :].bitcast(FP8), func=ACT.Copy, scale=sc[:, j : j + 1]
-            )
+            if j in WIDEN_ON_VECTOR:
+                nc.vector.tensor_scalar(
+                    out=planes[i][:, j, :],
+                    in0=raw[i][:, j, :].bitcast(FP8),
+                    scalar1=sc[:, j : j + 1],
+                    scalar2=None,
+                    op0=ALU.mult,
+                )
+            else:
+                nc.scalar.activation(
+                    out=planes[i][:, j, :], in_=raw[i][:, j, :].bitcast(FP8), func=ACT.Copy, scale=sc[:, j : j + 1]
+                )
 
         def interleave(i, half):
             if half == 0:
@@ -180,11 +200,16 @@ def tile_plelayer_pa_kernel(
             e0 = 4 * half
             nc.vector.tensor_copy(out=dst[:, :, e0 : e0 + 4, :], in_=src[:, :, e0 : e0 + 4, :])
 
-        def quantize(i):
-            cd = stage.tile([P, SLAB], U32, name="wcodes", tag="wcodes", bufs=3, align_bytes=64)
-            sl = stage.tile([P, SLAB], U8, name="wscl", tag="wscl", bufs=3, align_bytes=64)
-            nc.vector.quantize_mx(out=cd[:].bitcast(FP8X4), scales=sl[:], in_=grouped[i][:])
-            codes[i], scales[i] = cd, sl
+        def quantize(i, half):
+            if half == 0:
+                codes[i] = stage.tile([P, SLAB], U32, name="wcodes", tag="wcodes", bufs=3, align_bytes=64)
+                scales[i] = stage.tile([P, SLAB], U8, name="wscl", tag="wscl", bufs=3, align_bytes=64)
+            cols = slice(half * SLAB // 2, (half + 1) * SLAB // 2)
+            nc.vector.quantize_mx(
+                out=codes[i][:, cols].bitcast(FP8X4),
+                scales=scales[i][:, cols],
+                in_=grouped[i][:, half * 2 * SLAB : (half + 1) * 2 * SLAB],
+            )
 
         def mx_pass(out, cd, sl, e, rhs, rhs_scale):
             cols = slice(e * P, (e + 1) * P)
@@ -206,7 +231,7 @@ def tile_plelayer_pa_kernel(
             z = psum.tile([P, 2, B], F32, name="z", tag="z", bufs=3)
             banks[i] = z
             ops = []
-            if q in WARM:
+            if q in WARM or i < 3:
                 ops.append(lambda: mx_pass(z[:, 0, :], cd, sl, e0, xcodes[:], xscl[:]))
             ops.append(lambda: mx_pass(z[:, 0, :], cd, sl, e0, xcodes[:], xscl[:]))
             ops.append(lambda: mx_pass(z[:, 1, :], cd, sl, e0 + 1, xcodes[:], xscl[:]))
@@ -274,24 +299,23 @@ def tile_plelayer_pa_kernel(
                     out=both, in0=part[i][:].rearrange("p c s b -> p s c b"), in1=both, op=ALU.add
                 )
 
-        def store(uc, k):
+        def store(i):
+            uc, g = units[i]
+            if g == T:
+                return
             ot = sums[uc]
             ucols = slice(uc * P, (uc + 1) * P)
-            if k < 2:
-                rows = slice(k * P, (k + 1) * P)
-                fp = psum.tile([P, T, P], F32, name="fp", tag="misc", bufs=1)
-                for t in range(T):
-                    nc.tensor.transpose(fp[:, t, :], ot[:, t, rows], ident[:])
-                res = stage.tile([P, T, P], F32, name="res", tag="res", bufs=2)
-                nc.scalar.copy(out=res[:], in_=fp[:])
-                nc.sync.dma_start(out=out_0[:, rows, ucols].rearrange("t p u -> p t u"), in_=res[:])
-            else:
-                fs = psum.tile([P, 2, P], F32, name="fs", tag="misc", bufs=1)
+            done = (g, T) if g == T - 1 else (g,)
+            n = len(done)
+            fp = psum.tile([P, 2, 2, P], F32, name="fp", tag="misc", bufs=1)
+            for k in range(n):
                 for h in range(2):
-                    nc.tensor.transpose(fs[:, h, :], ot[:, T, h * P : (h + 1) * P], ident[:])
-                rs = stage.tile([P, 2, P], F32, name="rs", tag="rs", bufs=2)
-                nc.scalar.copy(out=rs[:], in_=fs[:])
-                nc.sync.dma_start(out=out_1.rearrange("(h p) u -> p h u", p=P)[:, :, ucols], in_=rs[:])
+                    nc.tensor.transpose(fp[:, k, h, :], ot[:, done[k], h * P : (h + 1) * P], ident[:])
+            res = stage.tile([P, 2, 2, P], F32, name="res", tag="res", bufs=2)
+            nc.scalar.copy(out=res[:, 0:n, :, :], in_=fp[:, 0:n, :, :])
+            nc.sync.dma_start(out=out_0[g].rearrange("(h p) u -> p h u", p=P)[:, :, ucols], in_=res[:, 0, :, :])
+            if n == 2:
+                nc.sync.dma_start(out=out_1.rearrange("(h p) u -> p h u", p=P)[:, :, ucols], in_=res[:, 1, :, :])
 
         def live(i):
             return 0 <= i < n_units
@@ -300,6 +324,11 @@ def tile_plelayer_pa_kernel(
             for s in range(-4, n_units + 4):
                 if live(s + 4):
                     load(s + 4)
+                if s == -4:
+                    load_scale()
+                if s == -3:
+                    load_biases()
+                    load_gates()
                 if live(s - 3):
                     add_up(s - 3)
                 for q in range(4):
@@ -307,6 +336,8 @@ def tile_plelayer_pa_kernel(
                         widen(s + 3, q)
                     if live(s + 2) and q % 2 == 0:
                         interleave(s + 2, q // 2)
+                        if s + 2 == 0:
+                            quantize(0, q // 2)
                     wide = expert_passes(s, q) if live(s) else []
                     thin = gate_passes(s - 2, q) if live(s - 2) else []
                     for n in range(4):
@@ -320,11 +351,11 @@ def tile_plelayer_pa_kernel(
                         gate_copy(s - 2, q)
                     if live(s - 1):
                         turn(s - 1, q)
-                    if live(s + 1) and q == 1:
-                        quantize(s + 1)
-                    if s in (0, 1):
-                        turn_gates(s, 4 * q)
-                    if live(s - 3) and (s - 3) % NG == NG - 1 and q < 3:
-                        store((s - 3) // NG, q)
-                if s == -1:
+                    if live(s + 1) and s + 1 > 0 and q % 2 == 1:
+                        quantize(s + 1, q // 2)
+                    if s in (1, 2):
+                        turn_gates(q % 2, 8 * (s - 1) + 4 * (q // 2))
+                    if live(s - 3) and q == 0:
+                        store(s - 3)
+                if s == -2:
                     build_gates()

@@ -25,9 +25,11 @@ BC = B // NB
 SLAB = P * E
 NSLOT = 13
 GROUP_ORDER = (T, 0, 1, 2, 3)
-WARM = (0, 1, 2, 3)
-TURN_ON_SCALAR = (1, 2, 3)
-WIDEN_ON_VECTOR = (1, 3)
+WIDEN_ON_VECTOR = (3,)
+UB = 32
+NF = P // UB
+EH = 4
+EL = 2
 
 
 def tile_plelayer_pa_kernel(
@@ -64,17 +66,29 @@ def tile_plelayer_pa_kernel(
         xscl = const.tile([P, B], U8, name="xscl", align_bytes=64)
         nc.vector.quantize_mx(out=xcodes[:].bitcast(FP8X4), scales=xscl[:], in_=xg[:])
 
-        bias_bf = const.tile([P, NG, UC, E], BF16, name="bias_bf")
-        bias_u = const.tile([P, NG, UC, E], F32, name="bias_u")
+        bias_rows = const.tile([P, UB * E], BF16, name="bias_rows")
+        bias_sorted = const.tile([P, EL, P], F32, name="bias_sorted")
+        bias_q = const.tile([P, EL, P], F32, name="bias_q")
+        nc.vector.memset(bias_rows[:], 0.0)
 
         def load_scale():
             nc.sync.dma_start(out=sc[:], in_=ew0_scale.rearrange("o (p j) a b -> p (o j a b)", j=PACK))
 
         def load_biases():
-            nc.sync.dma_start(out=bias_bf[:, T, :, :], in_=ebs0.rearrange("(c p) e -> p c e", p=P))
-            for t in range(T):
-                nc.sync.dma_start(out=bias_bf[:, t, :, :], in_=eb0[t].rearrange("(c p) e -> p c e", p=P))
-            nc.gpsimd.tensor_copy(out=bias_u[:], in_=bias_bf[:])
+            nc.sync.dma_start(out=bias_rows[0 : T * UC * NF, :], in_=eb0.rearrange("t (r u) e -> (t r) (u e)", u=UB))
+            nc.sync.dma_start(
+                out=bias_rows[T * UC * NF : NG * UC * NF, :], in_=ebs0.rearrange("(r u) e -> r (u e)", u=UB)
+            )
+
+        def turn_biases():
+            nc.gpsimd.tensor_copy(
+                out=bias_sorted[:].rearrange("r l (h u) -> r l h u", h=EH),
+                in_=bias_rows[:].rearrange("r (u h l) -> r l h u", h=EH, l=EL),
+            )
+            bt = psum.tile([P, EL, P], F32, name="bt", tag="misc", bufs=1)
+            for l in range(EL):
+                nc.tensor.transpose(bt[:, l, :], bias_sorted[:, l, :], ident[:])
+            nc.vector.tensor_copy(out=bias_q[:], in_=bt[:])
 
         lg_t = const.tile([P, 2, 64], BF16, name="lg_t")
         lg_s = const.tile([P, 2, 40], BF16, name="lg_s")
@@ -160,7 +174,7 @@ def tile_plelayer_pa_kernel(
         units = [(uc, g) for uc in range(UC) for g in GROUP_ORDER]
         n_units = len(units)
         raw, planes, grouped, codes, scales, relu_out = {}, {}, {}, {}, {}, {}
-        turned, sums, part, banks = {}, {}, {}, {}
+        turned, sums, acc, banks = {}, {}, {}, {}
 
         def load(i):
             uc, g = units[i]
@@ -179,7 +193,7 @@ def tile_plelayer_pa_kernel(
                 return
             if j == 0:
                 planes[i] = stage.tile([P, PACK, SLAB], BF16, name="planes", tag="planes", bufs=3)
-            if j in WIDEN_ON_VECTOR:
+            if j in WIDEN_ON_VECTOR and i % 2 == 1:
                 nc.vector.tensor_scalar(
                     out=planes[i][:, j, :],
                     in0=raw[i][:, j, :].bitcast(FP8),
@@ -195,10 +209,9 @@ def tile_plelayer_pa_kernel(
         def interleave(i, half):
             if half == 0:
                 grouped[i] = stage.tile([P, PACK * SLAB], BF16, name="grp", tag="grp", bufs=2, align_bytes=64)
-            dst = grouped[i][:].rearrange("p (e u j) -> p u e j", e=E, j=PACK)
-            src = planes[i][:].rearrange("p j (u e) -> p u e j", e=E)
-            e0 = 4 * half
-            nc.vector.tensor_copy(out=dst[:, :, e0 : e0 + 4, :], in_=src[:, :, e0 : e0 + 4, :])
+            dst = grouped[i][:].rearrange("p (l f h u j) -> p l f u h j", l=EL, f=NF, h=EH, j=PACK)
+            src = planes[i][:].rearrange("p j (f u h l) -> p l f u h j", f=NF, h=EH, l=EL)
+            nc.vector.tensor_copy(out=dst[:, half], in_=src[:, half])
 
         def quantize(i, half):
             if half == 0:
@@ -226,13 +239,11 @@ def tile_plelayer_pa_kernel(
         def expert_passes(i, q):
             cd, sl = codes[i], scales[i]
             if q == 0:
-                relu_out[i] = stage.tile([P, BC, E, NB], F32, name="hs", tag="hs", bufs=2)
+                relu_out[i] = stage.tile([P, BC, NF, EL, NB], F32, name="hs", tag="hs", bufs=2, align_bytes=64)
             e0 = 2 * q
             z = psum.tile([P, 2, B], F32, name="z", tag="z", bufs=3)
             banks[i] = z
             ops = []
-            if q in WARM or i < 3:
-                ops.append(lambda: mx_pass(z[:, 0, :], cd, sl, e0, xcodes[:], xscl[:]))
             ops.append(lambda: mx_pass(z[:, 0, :], cd, sl, e0, xcodes[:], xscl[:]))
             ops.append(lambda: mx_pass(z[:, 1, :], cd, sl, e0 + 1, xcodes[:], xscl[:]))
             return ops
@@ -240,72 +251,61 @@ def tile_plelayer_pa_kernel(
         def expert_relu(i, q):
             uc, g = units[i]
             for k in range(2):
-                e = 2 * q + k
+                l, f = divmod(2 * q + k, NF)
+                row = g * UC * NF + uc * NF + f
                 nc.scalar.activation(
-                    out=relu_out[i][:, :, e, :],
+                    out=relu_out[i][:, :, f, l, :],
                     in_=banks[i][:, k, :].rearrange("p (c b) -> p c b", b=NB),
                     func=ACT.Relu,
-                    bias=bias_u[:, g, uc, e : e + 1],
+                    bias=bias_q[:, l, row : row + 1],
                     scale=1.0,
                 )
 
         def turn(i, q):
             if q == 0:
-                turned[i] = stage.tile([P, BC, P], F32, name="ht", tag="ht", bufs=3)
-            hs, ht = relu_out[i], turned[i]
-            tp = psum.tile([P, 4, P], F32, name="tp", tag="tp", bufs=2)
-            for k in range(4):
-                nc.tensor.transpose(tp[:, k, :], hs[:, 4 * q + k, :, :].rearrange("p e b -> p (e b)"), ident[:])
-            if q in TURN_ON_SCALAR:
-                nc.scalar.copy(out=ht[:, 4 * q : 4 * q + 4, :], in_=tp[:])
-            else:
-                nc.vector.tensor_copy(out=ht[:, 4 * q : 4 * q + 4, :], in_=tp[:])
-
-        def gate_pass(out, ht, bc, s0, s1):
-            nc.tensor.matmul(
-                out=out.rearrange("p s b -> p (s b)"),
-                lhsT=ht[:, bc, :],
-                rhs=dall[:, bc, s0:s1, :].rearrange("p s b -> p (s b)"),
-                start=True,
-                stop=True,
+                turned[i] = stage.tile([P, BC, P], F32, name="ht", tag="ht", bufs=3, align_bytes=64)
+            nc.vector.transpose(
+                out=turned[i][:, 4 * q : 4 * q + 4, :].rearrange("p c u -> p (c u)"),
+                in_=relu_out[i][:, 4 * q : 4 * q + 4, :, :, :].rearrange("p c f l b -> p (c f l b)"),
             )
+
+        def gate_pass(out, ht, bc, s0, s1, start, stop):
+            nc.tensor.matmul(out=out, lhsT=ht[:, bc, :], rhs=dall[:, bc, s0:s1, :], start=start, stop=stop)
 
         def gate_passes(i, q):
             uc, g = units[i]
             ht = turned[i]
             if g == T:
+                acc[q] = psum.tile([P, 4, 8, NB], F32, name="acc%d" % q, tag="acc%d" % q, bufs=1)
+                a = acc[q]
+                return [
+                    lambda k=k: gate_pass(a[:, k, 0:NG, :], ht, 4 * q + k, 0, NG, k == 0, False) for k in range(4)
+                ]
+            a = acc[q]
+            return [
+                lambda k=k: gate_pass(
+                    a[:, k, g : NG : T - g, :], ht, 4 * q + k, 5 + 2 * g, 7 + 2 * g, False, g == T - 1 and k == 3
+                )
+                for k in range(4)
+            ]
+
+        def acc_copy(i, q):
+            uc, g = units[i]
+            if g == T - 1:
                 if q == 0:
                     sums[uc] = stage.tile([P, NG, B], F32, name="ot", tag="ot", bufs=2)
-                o = psum.tile([P, 4, NG, NB], F32, name="o", tag="o", bufs=2)
-                part[i] = o
-                return [lambda k=k: gate_pass(o[:, k, :, :], ht, 4 * q + k, 0, NG) for k in range(4)]
-            if q == 0:
-                part[i] = psum.tile([P, BC, 2, NB], F32, name="o", tag="o", bufs=2)
-            o = part[i]
-            return [lambda k=k: gate_pass(o[:, 4 * q + k, :, :], ht, 4 * q + k, 5 + 2 * g, 7 + 2 * g) for k in range(4)]
-
-        def gate_copy(i, q):
-            uc, g = units[i]
-            if g == T:
-                nc.vector.tensor_copy(
-                    out=sums[uc][:, :, 64 * q : 64 * q + 64].rearrange("p j (k b) -> p k j b", b=NB), in_=part[i][:]
+                nc.scalar.copy(
+                    out=sums[uc][:, :, 64 * q : 64 * q + 64].rearrange("p j (k b) -> p k j b", b=NB),
+                    in_=acc[q][:, :, 0:NG, :],
                 )
 
-        def add_up(i):
+        def store(i, r):
             uc, g = units[i]
-            if g != T:
-                both = sums[uc][:, g : NG : T - g, :].rearrange("p s (c b) -> p s c b", b=NB)
-                nc.vector.tensor_tensor(
-                    out=both, in0=part[i][:].rearrange("p c s b -> p s c b"), in1=both, op=ALU.add
-                )
-
-        def store(i):
-            uc, g = units[i]
-            if g == T:
+            if g != T - 1:
                 return
             ot = sums[uc]
             ucols = slice(uc * P, (uc + 1) * P)
-            done = (g, T) if g == T - 1 else (g,)
+            done = ((0, 1), (2, 3), (T,))[r]
             n = len(done)
             fp = psum.tile([P, 2, 2, P], F32, name="fp", tag="misc", bufs=1)
             for k in range(n):
@@ -313,9 +313,9 @@ def tile_plelayer_pa_kernel(
                     nc.tensor.transpose(fp[:, k, h, :], ot[:, done[k], h * P : (h + 1) * P], ident[:])
             res = stage.tile([P, 2, 2, P], F32, name="res", tag="res", bufs=2)
             nc.scalar.copy(out=res[:, 0:n, :, :], in_=fp[:, 0:n, :, :])
-            nc.sync.dma_start(out=out_0[g].rearrange("(h p) u -> p h u", p=P)[:, :, ucols], in_=res[:, 0, :, :])
-            if n == 2:
-                nc.sync.dma_start(out=out_1.rearrange("(h p) u -> p h u", p=P)[:, :, ucols], in_=res[:, 1, :, :])
+            for k in range(n):
+                dest = out_1 if done[k] == T else out_0[done[k]]
+                nc.sync.dma_start(out=dest.rearrange("(h p) u -> p h u", p=P)[:, :, ucols], in_=res[:, k, :, :])
 
         def live(i):
             return 0 <= i < n_units
@@ -326,11 +326,10 @@ def tile_plelayer_pa_kernel(
                     load(s + 4)
                 if s == -4:
                     load_scale()
-                if s == -3:
                     load_biases()
+                if s == -3:
                     load_gates()
-                if live(s - 3):
-                    add_up(s - 3)
+                    turn_biases()
                 for q in range(4):
                     if live(s + 3):
                         widen(s + 3, q)
@@ -348,14 +347,14 @@ def tile_plelayer_pa_kernel(
                     if live(s):
                         expert_relu(s, q)
                     if live(s - 2):
-                        gate_copy(s - 2, q)
+                        acc_copy(s - 2, q)
                     if live(s - 1):
                         turn(s - 1, q)
                     if live(s + 1) and s + 1 > 0 and q % 2 == 1:
                         quantize(s + 1, q // 2)
                     if s in (1, 2):
                         turn_gates(q % 2, 8 * (s - 1) + 4 * (q // 2))
-                    if live(s - 3) and q == 0:
-                        store(s - 3)
+                    if live(s - 3) and q < 3:
+                        store(s - 3, q)
                 if s == -2:
                     build_gates()

@@ -25,7 +25,8 @@ BC = B // NB
 SLAB = P * E
 NSLOT = 13
 GROUP_ORDER = (T, 0, 1, 2, 3)
-WIDEN_ON_VECTOR = (3,)
+TURN_ON_VECTOR = (0, 2)
+ACC = 6
 UB = 32
 NF = P // UB
 EH = 4
@@ -52,7 +53,7 @@ def tile_plelayer_pa_kernel(
         nc.sync.dma_start(out=x_sb[:], in_=x.rearrange("(h p) d -> p h d", p=P))
         sc = const.tile([P, PACK], F32, name="sc")
 
-        xt = psum.tile([P, 2, 2, P], F32, name="xt", tag="misc", bufs=1)
+        xt = psum.tile([P, 2, 2, P], F32, name="xt", tag="tp", bufs=2)
         for h in range(2):
             words = x_sb[:, h, :].bitcast(F32)
             for w in range(2):
@@ -70,6 +71,8 @@ def tile_plelayer_pa_kernel(
         bias_sorted = const.tile([P, EL, P], F32, name="bias_sorted")
         bias_q = const.tile([P, EL, P], F32, name="bias_q")
         nc.vector.memset(bias_rows[:], 0.0)
+        bias_bf = const.tile([P, NG, UC, E], BF16, name="bias_bf")
+        bias_u = const.tile([P, NG, UC, E], F32, name="bias_u")
 
         def load_scale():
             nc.sync.dma_start(out=sc[:], in_=ew0_scale.rearrange("o (p j) a b -> p (o j a b)", j=PACK))
@@ -80,12 +83,17 @@ def tile_plelayer_pa_kernel(
                 out=bias_rows[T * UC * NF : NG * UC * NF, :], in_=ebs0.rearrange("(r u) e -> r (u e)", u=UB)
             )
 
+            nc.sync.dma_start(out=bias_bf[:, T, :, :], in_=ebs0.rearrange("(c p) e -> p c e", p=P))
+            for t in range(T):
+                nc.sync.dma_start(out=bias_bf[:, t, :, :], in_=eb0[t].rearrange("(c p) e -> p c e", p=P))
+
         def turn_biases():
+            nc.gpsimd.tensor_copy(out=bias_u[:], in_=bias_bf[:])
             nc.gpsimd.tensor_copy(
                 out=bias_sorted[:].rearrange("r l (h u) -> r l h u", h=EH),
                 in_=bias_rows[:].rearrange("r (u h l) -> r l h u", h=EH, l=EL),
             )
-            bt = psum.tile([P, EL, P], F32, name="bt", tag="misc", bufs=1)
+            bt = psum.tile([P, EL, P], F32, name="bt", tag="tp", bufs=2)
             for l in range(EL):
                 nc.tensor.transpose(bt[:, l, :], bias_sorted[:, l, :], ident[:])
             nc.vector.tensor_copy(out=bias_q[:], in_=bt[:])
@@ -161,7 +169,7 @@ def tile_plelayer_pa_kernel(
 
         def turn_gates(h, s0):
             n = min(4, NSLOT - s0)
-            dps = psum.tile([P, 4, P], F32, name="dps", tag="misc", bufs=1)
+            dps = psum.tile([P, 4, P], F32, name="dps", tag="tp", bufs=2)
             for i in range(n):
                 nc.tensor.transpose(
                     dps[:, i, :], spread[h][:, s0 + i, :, :].rearrange("p e b -> p (e b)"), ident[:]
@@ -193,7 +201,7 @@ def tile_plelayer_pa_kernel(
                 return
             if j == 0:
                 planes[i] = stage.tile([P, PACK, SLAB], BF16, name="planes", tag="planes", bufs=3)
-            if j in WIDEN_ON_VECTOR and i % 2 == 1:
+            if j == 3 or (j == 1 and units[i][1] not in TURN_ON_VECTOR):
                 nc.vector.tensor_scalar(
                     out=planes[i][:, j, :],
                     in0=raw[i][:, j, :].bitcast(FP8),
@@ -209,8 +217,12 @@ def tile_plelayer_pa_kernel(
         def interleave(i, half):
             if half == 0:
                 grouped[i] = stage.tile([P, PACK * SLAB], BF16, name="grp", tag="grp", bufs=2, align_bytes=64)
-            dst = grouped[i][:].rearrange("p (l f h u j) -> p l f u h j", l=EL, f=NF, h=EH, j=PACK)
-            src = planes[i][:].rearrange("p j (f u h l) -> p l f u h j", f=NF, h=EH, l=EL)
+            if units[i][1] in TURN_ON_VECTOR:
+                dst = grouped[i][:].rearrange("p (l f h u j) -> p l f u h j", l=EL, f=NF, h=EH, j=PACK)
+                src = planes[i][:].rearrange("p j (f u h l) -> p l f u h j", f=NF, h=EH, l=EL)
+            else:
+                dst = grouped[i][:].rearrange("p (l h u j) -> p l u h j", l=EL, h=EH, j=PACK)
+                src = planes[i][:].rearrange("p j (u l h) -> p l u h j", l=EL, h=EH)
             nc.vector.tensor_copy(out=dst[:, half], in_=src[:, half])
 
         def quantize(i, half):
@@ -239,7 +251,7 @@ def tile_plelayer_pa_kernel(
         def expert_passes(i, q):
             cd, sl = codes[i], scales[i]
             if q == 0:
-                relu_out[i] = stage.tile([P, BC, NF, EL, NB], F32, name="hs", tag="hs", bufs=2, align_bytes=64)
+                relu_out[i] = stage.tile([P, BC, P], F32, name="hs", tag="hs", bufs=2, align_bytes=64)
             e0 = 2 * q
             z = psum.tile([P, 2, B], F32, name="z", tag="z", bufs=3)
             banks[i] = z
@@ -251,23 +263,37 @@ def tile_plelayer_pa_kernel(
         def expert_relu(i, q):
             uc, g = units[i]
             for k in range(2):
-                l, f = divmod(2 * q + k, NF)
-                row = g * UC * NF + uc * NF + f
+                if g in TURN_ON_VECTOR:
+                    l, f = divmod(2 * q + k, NF)
+                    row = g * UC * NF + uc * NF + f
+                    dest = relu_out[i][:].rearrange("p c (f l b) -> p c f l b", f=NF, l=EL)[:, :, f, l, :]
+                    bias = bias_q[:, l, row : row + 1]
+                else:
+                    e = 2 * q + k
+                    dest = relu_out[i][:].rearrange("p c (e b) -> p c e b", e=E)[:, :, e, :]
+                    bias = bias_u[:, g, uc, e : e + 1]
                 nc.scalar.activation(
-                    out=relu_out[i][:, :, f, l, :],
+                    out=dest,
                     in_=banks[i][:, k, :].rearrange("p (c b) -> p c b", b=NB),
                     func=ACT.Relu,
-                    bias=bias_q[:, l, row : row + 1],
+                    bias=bias,
                     scale=1.0,
                 )
 
         def turn(i, q):
             if q == 0:
                 turned[i] = stage.tile([P, BC, P], F32, name="ht", tag="ht", bufs=3, align_bytes=64)
-            nc.vector.transpose(
-                out=turned[i][:, 4 * q : 4 * q + 4, :].rearrange("p c u -> p (c u)"),
-                in_=relu_out[i][:, 4 * q : 4 * q + 4, :, :, :].rearrange("p c f l b -> p (c f l b)"),
-            )
+            hs, ht = relu_out[i], turned[i]
+            if units[i][1] in TURN_ON_VECTOR:
+                nc.vector.transpose(
+                    out=ht[:, 4 * q : 4 * q + 4, :].rearrange("p c u -> p (c u)"),
+                    in_=hs[:, 4 * q : 4 * q + 4, :].rearrange("p c k -> p (c k)"),
+                )
+            else:
+                tp = psum.tile([P, 4, P], F32, name="tp", tag="tp", bufs=2)
+                for k in range(4):
+                    nc.tensor.transpose(tp[:, k, :], hs[:, 4 * q + k, :], ident[:])
+                nc.scalar.copy(out=ht[:, 4 * q : 4 * q + 4, :], in_=tp[:])
 
         def gate_pass(out, ht, bc, s0, s1, start, stop):
             nc.tensor.matmul(out=out, lhsT=ht[:, bc, :], rhs=dall[:, bc, s0:s1, :], start=start, stop=stop)
@@ -275,29 +301,36 @@ def tile_plelayer_pa_kernel(
         def gate_passes(i, q):
             uc, g = units[i]
             ht = turned[i]
-            if g == T:
-                acc[q] = psum.tile([P, 4, 8, NB], F32, name="acc%d" % q, tag="acc%d" % q, bufs=1)
-                a = acc[q]
-                return [
-                    lambda k=k: gate_pass(a[:, k, 0:NG, :], ht, 4 * q + k, 0, NG, k == 0, False) for k in range(4)
-                ]
-            a = acc[q]
-            return [
-                lambda k=k: gate_pass(
-                    a[:, k, g : NG : T - g, :], ht, 4 * q + k, 5 + 2 * g, 7 + 2 * g, False, g == T - 1 and k == 3
-                )
-                for k in range(4)
-            ]
+            ops = []
+            for bc in range(4 * q, 4 * q + 4):
+                bank, k = divmod(bc, ACC)
+                if g == T and k == 0:
+                    acc[bank] = psum.tile([P, 512], F32, name="acc%d" % bank, tag="acc%d" % bank, bufs=1)
+                a = acc[bank][:, 0 : ACC * NG * NB].rearrange("p (k j b) -> p k j b", j=NG, b=NB)
+                if g == T:
+                    ops.append(lambda a=a, k=k, bc=bc: gate_pass(a[:, k, :, :], ht, bc, 0, NG, k == 0, False))
+                else:
+                    last = g == T - 1 and (k == ACC - 1 or bc == BC - 1)
+                    ops.append(
+                        lambda a=a, k=k, bc=bc, last=last: gate_pass(
+                            a[:, k, g : NG : T - g, :], ht, bc, 5 + 2 * g, 7 + 2 * g, False, last
+                        )
+                    )
+            return ops
 
         def acc_copy(i, q):
             uc, g = units[i]
-            if g == T - 1:
-                if q == 0:
-                    sums[uc] = stage.tile([P, NG, B], F32, name="ot", tag="ot", bufs=2)
-                nc.scalar.copy(
-                    out=sums[uc][:, :, 64 * q : 64 * q + 64].rearrange("p j (k b) -> p k j b", b=NB),
-                    in_=acc[q][:, :, 0:NG, :],
-                )
+            if g != T - 1 or q == 0:
+                return
+            bank = q - 1
+            if bank == 0:
+                sums[uc] = stage.tile([P, NG, B], F32, name="ot", tag="ot", bufs=2)
+            n = min(ACC, BC - ACC * bank)
+            a = acc[bank][:, 0 : ACC * NG * NB].rearrange("p (k j b) -> p k j b", j=NG, b=NB)
+            nc.scalar.copy(
+                out=sums[uc][:, :, ACC * NB * bank : ACC * NB * bank + n * NB].rearrange("p j (k b) -> p k j b", b=NB),
+                in_=a[:, 0:n, :, :],
+            )
 
         def store(i, r):
             uc, g = units[i]
@@ -307,7 +340,7 @@ def tile_plelayer_pa_kernel(
             ucols = slice(uc * P, (uc + 1) * P)
             done = ((0, 1), (2, 3), (T,))[r]
             n = len(done)
-            fp = psum.tile([P, 2, 2, P], F32, name="fp", tag="misc", bufs=1)
+            fp = psum.tile([P, 2, 2, P], F32, name="fp", tag="tp", bufs=2)
             for k in range(n):
                 for h in range(2):
                     nc.tensor.transpose(fp[:, k, h, :], ot[:, done[k], h * P : (h + 1) * P], ident[:])

@@ -256,8 +256,8 @@ def tile_plelayer_pa_kernel(
             z = psum.tile([P, 2, B], F32, name="z", tag="z", bufs=3)
             banks[i] = z
             ops = []
-            ops.append(lambda: mx_pass(z[:, 0, :], cd, sl, e0, xcodes[:], xscl[:]))
-            ops.append(lambda: mx_pass(z[:, 1, :], cd, sl, e0 + 1, xcodes[:], xscl[:]))
+            for k in (0, 0, 1):
+                ops.append(lambda k=k: mx_pass(z[:, k, :], cd, sl, e0 + k, xcodes[:], xscl[:]))
             return ops
 
         def expert_relu(i, q):

@@ -201,7 +201,7 @@ def tile_plelayer_pa_kernel(
                 return
             if j == 0:
                 planes[i] = stage.tile([P, PACK, SLAB], BF16, name="planes", tag="planes", bufs=3)
-            if j == 3 or (j == 1 and units[i][1] not in TURN_ON_VECTOR):
+            if j in (1, 3) or (j == 2 and units[i][1] not in TURN_ON_VECTOR):
                 nc.vector.tensor_scalar(
                     out=planes[i][:, j, :],
                     in0=raw[i][:, j, :].bitcast(FP8),

@@ -201,18 +201,13 @@ def tile_plelayer_pa_kernel(
                 return
             if j == 0:
                 planes[i] = stage.tile([P, PACK, SLAB], BF16, name="planes", tag="planes", bufs=3)
-            if j in (1, 3) or (j == 2 and units[i][1] not in TURN_ON_VECTOR):
-                nc.vector.tensor_scalar(
-                    out=planes[i][:, j, :],
-                    in0=raw[i][:, j, :].bitcast(FP8),
-                    scalar1=sc[:, j : j + 1],
-                    scalar2=None,
-                    op0=ALU.mult,
-                )
-            else:
-                nc.scalar.activation(
-                    out=planes[i][:, j, :], in_=raw[i][:, j, :].bitcast(FP8), func=ACT.Copy, scale=sc[:, j : j + 1]
-                )
+            nc.vector.tensor_scalar(
+                out=planes[i][:, j, :],
+                in0=raw[i][:, j, :].bitcast(FP8),
+                scalar1=sc[:, j : j + 1],
+                scalar2=None,
+                op0=ALU.mult,
+            )
 
         def interleave(i, half):
             if half == 0:
@@ -223,7 +218,10 @@ def tile_plelayer_pa_kernel(
             else:
                 dst = grouped[i][:].rearrange("p (l h u j) -> p l u h j", l=EL, h=EH, j=PACK)
                 src = planes[i][:].rearrange("p j (u l h) -> p l u h j", l=EL, h=EH)
-            nc.vector.tensor_copy(out=dst[:, half], in_=src[:, half])
+            if half == 1 and units[i][1] not in TURN_ON_VECTOR:
+                nc.scalar.copy(out=dst[:, half], in_=src[:, half])
+            else:
+                nc.vector.tensor_copy(out=dst[:, half], in_=src[:, half])
 
         def quantize(i, half):
             if half == 0:

@@ -87,16 +87,18 @@ def tile_plelayer_pa_kernel(
             for t in range(T):
                 nc.sync.dma_start(out=bias_bf[:, t, :, :], in_=eb0[t].rearrange("(c p) e -> p c e", p=P))
 
-        def turn_biases():
+        def cast_biases():
             nc.gpsimd.tensor_copy(out=bias_u[:], in_=bias_bf[:])
             nc.gpsimd.tensor_copy(
                 out=bias_sorted[:].rearrange("r l (h u) -> r l h u", h=EH),
                 in_=bias_rows[:].rearrange("r (u h l) -> r l h u", h=EH, l=EL),
             )
+
+        def turn_biases():
             bt = psum.tile([P, EL, P], F32, name="bt", tag="tp", bufs=2)
             for l in range(EL):
                 nc.tensor.transpose(bt[:, l, :], bias_sorted[:, l, :], ident[:])
-            nc.vector.tensor_copy(out=bias_q[:], in_=bt[:])
+            nc.scalar.copy(out=bias_q[:], in_=bt[:])
 
         lg_t = const.tile([P, 2, 64], BF16, name="lg_t")
         lg_s = const.tile([P, 2, 40], BF16, name="lg_s")
@@ -174,7 +176,7 @@ def tile_plelayer_pa_kernel(
                 nc.tensor.transpose(
                     dps[:, i, :], spread[h][:, s0 + i, :, :].rearrange("p e b -> p (e b)"), ident[:]
                 )
-            nc.vector.tensor_copy(
+            nc.scalar.copy(
                 out=dall[:, 8 * h : 8 * h + 8, s0 : s0 + n, :].rearrange("p c s b -> p s c b"),
                 in_=dps[:, 0:n, :].rearrange("p s (c b) -> p s c b", b=NB),
             )
@@ -201,13 +203,18 @@ def tile_plelayer_pa_kernel(
                 return
             if j == 0:
                 planes[i] = stage.tile([P, PACK, SLAB], BF16, name="planes", tag="planes", bufs=3)
-            nc.vector.tensor_scalar(
-                out=planes[i][:, j, :],
-                in0=raw[i][:, j, :].bitcast(FP8),
-                scalar1=sc[:, j : j + 1],
-                scalar2=None,
-                op0=ALU.mult,
-            )
+            if j == 3 or (j > 0 and units[i][1] not in TURN_ON_VECTOR):
+                nc.vector.tensor_scalar(
+                    out=planes[i][:, j, :],
+                    in0=raw[i][:, j, :].bitcast(FP8),
+                    scalar1=sc[:, j : j + 1],
+                    scalar2=None,
+                    op0=ALU.mult,
+                )
+            else:
+                nc.scalar.activation(
+                    out=planes[i][:, j, :], in_=raw[i][:, j, :].bitcast(FP8), func=ACT.Copy, scale=sc[:, j : j + 1]
+                )
 
         def interleave(i, half):
             if half == 0:
@@ -218,10 +225,7 @@ def tile_plelayer_pa_kernel(
             else:
                 dst = grouped[i][:].rearrange("p (l h u j) -> p l u h j", l=EL, h=EH, j=PACK)
                 src = planes[i][:].rearrange("p j (u l h) -> p l u h j", l=EL, h=EH)
-            if half == 1 and units[i][1] not in TURN_ON_VECTOR:
-                nc.scalar.copy(out=dst[:, half], in_=src[:, half])
-            else:
-                nc.vector.tensor_copy(out=dst[:, half], in_=src[:, half])
+            nc.vector.tensor_copy(out=dst[:, half], in_=src[:, half])
 
         def quantize(i, half):
             if half == 0:
@@ -357,17 +361,20 @@ def tile_plelayer_pa_kernel(
                     load(s + 4)
                 if s == -4:
                     load_scale()
-                    load_biases()
                 if s == -3:
+                    load_biases()
+                    cast_biases()
+                if s == -2:
                     load_gates()
+                if s == -1:
                     turn_biases()
                 for q in range(4):
-                    if live(s + 3):
-                        widen(s + 3, q)
                     if live(s + 2) and q % 2 == 0:
                         interleave(s + 2, q // 2)
                         if s + 2 == 0:
                             quantize(0, q // 2)
+                    if live(s + 3):
+                        widen(s + 3, q)
                     wide = expert_passes(s, q) if live(s) else []
                     thin = gate_passes(s - 2, q) if live(s - 2) else []
                     for n in range(4):

@@ -26,6 +26,7 @@ SLAB = P * E
 NSLOT = 13
 GROUP_ORDER = (T, 0, 1, 2, 3)
 TURN_ON_VECTOR = (0, 2)
+CFG = {"vkind": None, "vwiden": None, "repeats": (0, 0, 1), "run": 8, "bufs": {"hs": 3, "res": 3}, "pin": "PE", "o_turn": 4, "o_gate": 8, "o_store": 12, "early_gates": False, "tail": 0, "repeat_rule": "heavy", "q_same_step": False, "bytes_first": False}
 ACC = 6
 UB = 32
 NF = P // UB
@@ -37,6 +38,10 @@ def tile_plelayer_pa_kernel(
     tc, x, ews0, ebs0, ew0_bytes, ew0_scale, eb0, gate_pre0, gb0, sgate_pre, gbs, out_0, out_1
 ):
     nc = tc.nc
+
+    def nbufs(tag, n):
+        return CFG["bufs"].get(tag, n)
+
     with ExitStack() as ctx:
         const = ctx.enter_context(tc.tile_pool(name="const", bufs=1))
         stage = ctx.enter_context(tc.tile_pool(name="stage", bufs=2))
@@ -53,7 +58,7 @@ def tile_plelayer_pa_kernel(
         nc.sync.dma_start(out=x_sb[:], in_=x.rearrange("(h p) d -> p h d", p=P))
         sc = const.tile([P, PACK], F32, name="sc")
 
-        xt = psum.tile([P, 2, 2, P], F32, name="xt", tag="tp", bufs=2)
+        xt = psum.tile([P, 2, 2, P], F32, name="xt", tag="tp", bufs=nbufs("tp", 2))
         for h in range(2):
             words = x_sb[:, h, :].bitcast(F32)
             for w in range(2):
@@ -95,7 +100,7 @@ def tile_plelayer_pa_kernel(
             )
 
         def turn_biases():
-            bt = psum.tile([P, EL, P], F32, name="bt", tag="tp", bufs=2)
+            bt = psum.tile([P, EL, P], F32, name="bt", tag="tp", bufs=nbufs("tp", 2))
             for l in range(EL):
                 nc.tensor.transpose(bt[:, l, :], bias_sorted[:, l, :], ident[:])
             nc.scalar.copy(out=bias_q[:], in_=bt[:])
@@ -171,7 +176,7 @@ def tile_plelayer_pa_kernel(
 
         def turn_gates(h, s0):
             n = min(4, NSLOT - s0)
-            dps = psum.tile([P, 4, P], F32, name="dps", tag="tp", bufs=2)
+            dps = psum.tile([P, 4, P], F32, name="dps", tag="tp", bufs=nbufs("tp", 2))
             for i in range(n):
                 nc.tensor.transpose(
                     dps[:, i, :], spread[h][:, s0 + i, :, :].rearrange("p e b -> p (e b)"), ident[:]
@@ -183,6 +188,16 @@ def tile_plelayer_pa_kernel(
 
         units = [(uc, g) for uc in range(UC) for g in GROUP_ORDER]
         n_units = len(units)
+
+        def vkind(i):
+            if CFG["vkind"] is not None:
+                return i in CFG["vkind"]
+            return units[i][1] in TURN_ON_VECTOR
+
+        def vwiden(i, j):
+            if CFG["vwiden"] is not None:
+                return j in CFG["vwiden"][i]
+            return j == 3 or (j > 0 and not vkind(i))
         raw, planes, grouped, codes, scales, relu_out = {}, {}, {}, {}, {}, {}
         turned, sums, acc, banks = {}, {}, {}, {}
 
@@ -190,11 +205,11 @@ def tile_plelayer_pa_kernel(
             uc, g = units[i]
             cols = slice(uc * SLAB, (uc + 1) * SLAB)
             if g == T:
-                pl = stage.tile([P, PACK, SLAB], BF16, name="planes", tag="planes", bufs=3)
+                pl = stage.tile([P, PACK, SLAB], BF16, name="planes", tag="planes", bufs=nbufs("planes", 3))
                 nc.sync.dma_start(out=pl[:], in_=ews0.rearrange("(p j) u e -> p j (u e)", j=PACK)[:, :, cols])
                 planes[i] = pl
             else:
-                wb = stage.tile([P, PACK, SLAB], U8, name="wbytes", tag="wbytes", bufs=3)
+                wb = stage.tile([P, PACK, SLAB], U8, name="wbytes", tag="wbytes", bufs=nbufs("wbytes", 3))
                 nc.sync.dma_start(out=wb[:], in_=ew0_bytes[g].rearrange("(p j) u e -> p j (u e)", j=PACK)[:, :, cols])
                 raw[i] = wb
 
@@ -202,8 +217,8 @@ def tile_plelayer_pa_kernel(
             if units[i][1] == T:
                 return
             if j == 0:
-                planes[i] = stage.tile([P, PACK, SLAB], BF16, name="planes", tag="planes", bufs=3)
-            if j == 3 or (j > 0 and units[i][1] not in TURN_ON_VECTOR):
+                planes[i] = stage.tile([P, PACK, SLAB], BF16, name="planes", tag="planes", bufs=nbufs("planes", 3))
+            if vwiden(i, j):
                 nc.vector.tensor_scalar(
                     out=planes[i][:, j, :],
                     in0=raw[i][:, j, :].bitcast(FP8),
@@ -218,8 +233,8 @@ def tile_plelayer_pa_kernel(
 
         def interleave(i, half):
             if half == 0:
-                grouped[i] = stage.tile([P, PACK * SLAB], BF16, name="grp", tag="grp", bufs=2, align_bytes=64)
-            if units[i][1] in TURN_ON_VECTOR:
+                grouped[i] = stage.tile([P, PACK * SLAB], BF16, name="grp", tag="grp", bufs=nbufs("grp", 2), align_bytes=64)
+            if vkind(i):
                 dst = grouped[i][:].rearrange("p (l f h u j) -> p l f u h j", l=EL, f=NF, h=EH, j=PACK)
                 src = planes[i][:].rearrange("p j (f u h l) -> p l f u h j", f=NF, h=EH, l=EL)
             else:
@@ -229,8 +244,8 @@ def tile_plelayer_pa_kernel(
 
         def quantize(i, half):
             if half == 0:
-                codes[i] = stage.tile([P, SLAB], U32, name="wcodes", tag="wcodes", bufs=3, align_bytes=64)
-                scales[i] = stage.tile([P, SLAB], U8, name="wscl", tag="wscl", bufs=3, align_bytes=64)
+                codes[i] = stage.tile([P, SLAB], U32, name="wcodes", tag="wcodes", bufs=nbufs("wcodes", 3), align_bytes=64)
+                scales[i] = stage.tile([P, SLAB], U8, name="wscl", tag="wscl", bufs=nbufs("wscl", 3), align_bytes=64)
             cols = slice(half * SLAB // 2, (half + 1) * SLAB // 2)
             nc.vector.quantize_mx(
                 out=codes[i][:, cols].bitcast(FP8X4),
@@ -253,19 +268,22 @@ def tile_plelayer_pa_kernel(
         def expert_passes(i, q):
             cd, sl = codes[i], scales[i]
             if q == 0:
-                relu_out[i] = stage.tile([P, BC, P], F32, name="hs", tag="hs", bufs=2, align_bytes=64)
+                relu_out[i] = stage.tile([P, BC, P], F32, name="hs", tag="hs", bufs=nbufs("hs", 2), align_bytes=64)
             e0 = 2 * q
-            z = psum.tile([P, 2, B], F32, name="z", tag="z", bufs=3)
+            z = psum.tile([P, 2, B], F32, name="z", tag="z", bufs=nbufs("z", 3))
             banks[i] = z
             ops = []
-            for k in (0, 0, 1):
+            pattern = CFG["repeats"]
+            if live(i - 1) and CFG["repeat_rule"] == ("heavy" if vkind(i - 1) else "light"):
+                pattern = (0, 1)
+            for k in pattern:
                 ops.append(lambda k=k: mx_pass(z[:, k, :], cd, sl, e0 + k, xcodes[:], xscl[:]))
             return ops
 
         def expert_relu(i, q):
             uc, g = units[i]
             for k in range(2):
-                if g in TURN_ON_VECTOR:
+                if vkind(i):
                     l, f = divmod(2 * q + k, NF)
                     row = g * UC * NF + uc * NF + f
                     dest = relu_out[i][:].rearrange("p c (f l b) -> p c f l b", f=NF, l=EL)[:, :, f, l, :]
@@ -284,15 +302,15 @@ def tile_plelayer_pa_kernel(
 
         def turn(i, q):
             if q == 0:
-                turned[i] = stage.tile([P, BC, P], F32, name="ht", tag="ht", bufs=3, align_bytes=64)
+                turned[i] = stage.tile([P, BC, P], F32, name="ht", tag="ht", bufs=nbufs("ht", 3), align_bytes=64)
             hs, ht = relu_out[i], turned[i]
-            if units[i][1] in TURN_ON_VECTOR:
+            if vkind(i):
                 nc.vector.transpose(
                     out=ht[:, 4 * q : 4 * q + 4, :].rearrange("p c u -> p (c u)"),
                     in_=hs[:, 4 * q : 4 * q + 4, :].rearrange("p c k -> p (c k)"),
                 )
             else:
-                tp = psum.tile([P, 4, P], F32, name="tp", tag="tp", bufs=2)
+                tp = psum.tile([P, 4, P], F32, name="tp", tag="tp", bufs=nbufs("tp", 2))
                 for k in range(4):
                     nc.tensor.transpose(tp[:, k, :], hs[:, 4 * q + k, :], ident[:])
                 nc.scalar.copy(out=ht[:, 4 * q : 4 * q + 4, :], in_=tp[:])
@@ -326,7 +344,7 @@ def tile_plelayer_pa_kernel(
                 return
             bank = q - 1
             if bank == 0:
-                sums[uc] = stage.tile([P, NG, B], F32, name="ot", tag="ot", bufs=2)
+                sums[uc] = stage.tile([P, NG, B], F32, name="ot", tag="ot", bufs=nbufs("ot", 2))
             n = min(ACC, BC - ACC * bank)
             a = acc[bank][:, 0 : ACC * NG * NB].rearrange("p (k j b) -> p k j b", j=NG, b=NB)
             nc.scalar.copy(
@@ -342,11 +360,11 @@ def tile_plelayer_pa_kernel(
             ucols = slice(uc * P, (uc + 1) * P)
             done = ((0, 1), (2, 3), (T,))[r]
             n = len(done)
-            fp = psum.tile([P, 2, 2, P], F32, name="fp", tag="tp", bufs=2)
+            fp = psum.tile([P, 2, 2, P], F32, name="fp", tag="tp", bufs=nbufs("tp", 2))
             for k in range(n):
                 for h in range(2):
                     nc.tensor.transpose(fp[:, k, h, :], ot[:, done[k], h * P : (h + 1) * P], ident[:])
-            res = stage.tile([P, 2, 2, P], F32, name="res", tag="res", bufs=2)
+            res = stage.tile([P, 2, 2, P], F32, name="res", tag="res", bufs=nbufs("res", 2))
             nc.scalar.copy(out=res[:, 0:n, :, :], in_=fp[:, 0:n, :, :])
             for k in range(n):
                 dest = out_1 if done[k] == T else out_0[done[k]]
@@ -355,44 +373,80 @@ def tile_plelayer_pa_kernel(
         def live(i):
             return 0 <= i < n_units
 
-        with tc.manual_schedule(engines={mybir.EngineType.PE}):
-            for s in range(-4, n_units + 4):
-                if live(s + 4):
-                    load(s + 4)
-                if s == -4:
-                    load_scale()
-                if s == -3:
-                    load_biases()
-                    cast_biases()
-                if s == -2:
+        pins = {
+            "PE": {mybir.EngineType.PE},
+            "PE+ACT": {mybir.EngineType.PE, mybir.EngineType.Activation},
+            "PE+DVE": {mybir.EngineType.PE, mybir.EngineType.DVE},
+            "PE+ACT+DVE": {mybir.EngineType.PE, mybir.EngineType.Activation, mybir.EngineType.DVE},
+        }[CFG["pin"]]
+        o_turn, o_gate, o_store = CFG["o_turn"], CFG["o_gate"], CFG["o_store"]
+        gate_at = {}
+        t_last = 4 * (n_units - 1)
+        for i in range(n_units):
+            for q in range(4):
+                at = 4 * i + q + o_gate
+                if CFG["tail"] and at >= t_last:
+                    at = max(t_last + (at - t_last) // 2, at - CFG["tail"])
+                gate_at.setdefault(at, []).append((i, q))
+        if CFG["tail"]:
+            o_store = o_store - CFG["tail"]
+        with tc.manual_schedule(engines=pins):
+            for tau in range(-16, 4 * n_units + 8 + o_store):
+                s, q = divmod(tau, 4)
+                if tau == -16 and CFG["early_gates"]:
                     load_gates()
-                if s == -1:
-                    turn_biases()
-                for q in range(4):
-                    if live(s + 2) and q % 2 == 0:
-                        interleave(s + 2, q // 2)
-                        if s + 2 == 0:
-                            quantize(0, q // 2)
-                    if live(s + 3):
-                        widen(s + 3, q)
-                    wide = expert_passes(s, q) if live(s) else []
-                    thin = gate_passes(s - 2, q) if live(s - 2) else []
-                    for n in range(4):
-                        if n < len(thin):
-                            thin[n]()
-                        if n < len(wide):
-                            wide[n]()
-                    if live(s):
-                        expert_relu(s, q)
-                    if live(s - 2):
-                        acc_copy(s - 2, q)
-                    if live(s - 1):
-                        turn(s - 1, q)
-                    if live(s + 1) and s + 1 > 0 and q % 2 == 1:
-                        quantize(s + 1, q // 2)
-                    if s in (1, 2):
-                        turn_gates(q % 2, 8 * (s - 1) + 4 * (q // 2))
-                    if live(s - 3) and q < 3:
-                        store(s - 3, q)
-                if s == -2:
+                    build_gates()
+                if q == 0:
+                    if CFG["bytes_first"] and s == -4:
+                        load_scale()
+                        load(1)
+                    if live(s + 4) and not (CFG["bytes_first"] and s + 4 == 1):
+                        load(s + 4)
+                    if s == -4 and not CFG["bytes_first"]:
+                        load_scale()
+                    if s == -3:
+                        load_biases()
+                        cast_biases()
+                    if s == -2 and not CFG["early_gates"]:
+                        load_gates()
+                    if s == -1:
+                        turn_biases()
+                if live(s + 2) and q % 2 == 0:
+                    interleave(s + 2, q // 2)
+                    if s + 2 == 0 and not CFG["q_same_step"]:
+                        quantize(0, q // 2)
+                if live(s + 3):
+                    widen(s + 3, q)
+                ti, tq = divmod(tau - o_turn, 4)
+                si, sq = divmod(tau - o_store, 4)
+                wide = expert_passes(s, q) if live(s) else []
+                due = [iq for iq in gate_at.get(tau, ())]
+                thin = []
+                for gi, gq in due:
+                    thin.extend(gate_passes(gi, gq))
+                for n in range(max(len(thin), len(wide))):
+                    if n < len(thin):
+                        thin[n]()
+                    if n < len(wide):
+                        wide[n]()
+                if live(s):
+                    expert_relu(s, q)
+                for gi, gq in due:
+                    acc_copy(gi, gq)
+                if live(ti):
+                    if vkind(ti) or CFG["run"] == 4:
+                        turn(ti, tq)
+                    elif tq % 2 == 1:
+                        turn(ti, tq - 1)
+                        turn(ti, tq)
+                if CFG["q_same_step"]:
+                    if live(s + 2) and q % 2 == 1:
+                        quantize(s + 2, q // 2)
+                elif live(s + 1) and s + 1 > 0 and q % 2 == 1:
+                    quantize(s + 1, q // 2)
+                if s in (1, 2):
+                    turn_gates(q % 2, 8 * (s - 1) + 4 * (q // 2))
+                if live(si) and sq < 3:
+                    store(si, sq)
+                if s == -2 and q == 3 and not CFG["early_gates"]:
                     build_gates()

@@ -26,7 +26,7 @@ SLAB = P * E
 NSLOT = 13
 GROUP_ORDER = (T, 0, 1, 2, 3)
 TURN_ON_VECTOR = (0, 2)
-CFG = {"vkind": None, "vwiden": None, "repeats": (0, 0, 1), "run": 8, "bufs": {"hs": 3, "res": 3}, "pin": "PE", "o_turn": 4, "o_gate": 8, "o_store": 12, "early_gates": False, "tail": 0, "repeat_rule": "heavy", "q_same_step": False, "bytes_first": False}
+CFG = {"vkind": None, "vwiden": None, "repeats": (0, 0, 1), "run": 8, "bufs": {"hs": 3, "res": 3}, "pin": "PE", "o_turn": 4, "o_gate": 8, "o_store": 12, "early_gates": False, "tail": 0, "repeat_rule": "heavy", "q_same_step": False, "bytes_first": False, "tail_fill": (), "copy_order": "jh"}
 ACC = 6
 UB = 32
 NF = P // UB
@@ -240,6 +240,11 @@ def tile_plelayer_pa_kernel(
             else:
                 dst = grouped[i][:].rearrange("p (l h u j) -> p l u h j", l=EL, h=EH, j=PACK)
                 src = planes[i][:].rearrange("p j (u l h) -> p l u h j", l=EL, h=EH)
+            if CFG["copy_order"] == "jh":
+                if vkind(i):
+                    dst, src = dst.rearrange("p l f u h j -> p l f u j h"), src.rearrange("p l f u h j -> p l f u j h")
+                else:
+                    dst, src = dst.rearrange("p l u h j -> p l u j h"), src.rearrange("p l u h j -> p l u j h")
             nc.vector.tensor_copy(out=dst[:, half], in_=src[:, half])
 
         def quantize(i, half):
@@ -278,6 +283,14 @@ def tile_plelayer_pa_kernel(
                 pattern = (0, 1)
             for k in pattern:
                 ops.append(lambda k=k: mx_pass(z[:, k, :], cd, sl, e0 + k, xcodes[:], xscl[:]))
+            return ops
+
+        def filler_passes(q):
+            cd, sl = codes[n_units - 1], scales[n_units - 1]
+            z = psum.tile([P, 2, B], F32, name="z", tag="z", bufs=nbufs("z", 3))
+            ops = []
+            for k in CFG["tail_fill"]:
+                ops.append(lambda k=k: mx_pass(z[:, k, :], cd, sl, 2 * q + k, xcodes[:], xscl[:]))
             return ops
 
         def expert_relu(i, q):
@@ -421,6 +434,8 @@ def tile_plelayer_pa_kernel(
                 si, sq = divmod(tau - o_store, 4)
                 wide = expert_passes(s, q) if live(s) else []
                 due = [iq for iq in gate_at.get(tau, ())]
+                if s >= n_units and tau < 4 * (n_units - 1) + o_store + 3 and CFG["tail_fill"]:
+                    wide = filler_passes(q)
                 thin = []
                 for gi, gq in due:
                     thin.extend(gate_passes(gi, gq))

@@ -26,7 +26,7 @@ SLAB = P * E
 NSLOT = 13
 GROUP_ORDER = (T, 0, 1, 2, 3)
 TURN_ON_VECTOR = (0, 2)
-CFG = {"vkind": None, "vwiden": None, "repeats": (0, 0, 1), "run": 8, "bufs": {"hs": 3, "res": 3}, "pin": "PE", "o_turn": 4, "o_gate": 8, "o_store": 12, "early_gates": False, "tail": 0, "repeat_rule": "heavy", "q_same_step": False, "bytes_first": False, "tail_fill": (), "copy_order": "jh"}
+CFG = {"vkind": None, "vwiden": None, "repeats": (0, 0, 1), "run": 8, "bufs": {"hs": 3, "res": 3}, "pin": "PE", "o_turn": 4, "o_gate": 8, "o_store": 12, "early_gates": False, "tail": 0, "repeat_rule": "heavy", "q_same_step": False, "bytes_first": False, "tail_fill": (), "copy_order": "jh", "gb_by_pe": True}
 ACC = 6
 UB = 32
 NF = P // UB
@@ -107,8 +107,21 @@ def tile_plelayer_pa_kernel(
 
         lg_t = const.tile([P, 2, 64], BF16, name="lg_t")
         lg_s = const.tile([P, 2, 40], BF16, name="lg_s")
-        gb_t = const.tile([P, 64], BF16, name="gb_t")
-        gb_s = const.tile([P, 40], BF16, name="gb_s")
+        gate_bias = {}
+        if CFG["gb_by_pe"]:
+            gb_row = const.tile([P, 104], BF16, name="gb_row")
+            ones = const.tile([P, P], BF16, name="ones")
+            nc.vector.memset(gb_row[:], 0.0)
+            nc.vector.memset(ones[:], 1.0)
+            nc.sync.dma_start(out=gb_row[0:1, 0:64], in_=gb0.rearrange("(o t) k -> o (t k)", o=1))
+            nc.sync.dma_start(out=gb_row[0:1, 64:104], in_=gbs.rearrange("(o k) -> o k", o=1))
+            gbp = psum.tile([P, 104], F32, name="gbp", tag="tp", bufs=nbufs("tp", 2))
+            nc.tensor.matmul(out=gbp[:], lhsT=ones[:], rhs=gb_row[:], start=True, stop=True)
+            gate_bias["t"], gate_bias["s"] = gbp[:, 0:64], gbp[:, 64:104]
+        else:
+            gb_t = const.tile([P, 64], BF16, name="gb_t")
+            gb_s = const.tile([P, 40], BF16, name="gb_s")
+            gate_bias["t"], gate_bias["s"] = gb_t[:], gb_s[:]
 
         def load_gates():
             for h in range(2):
@@ -117,19 +130,21 @@ def tile_plelayer_pa_kernel(
                     in_=gate_pre0[:, h * P : (h + 1) * P, :].rearrange("t p k -> p t k"),
                 )
             nc.sync.dma_start(out=lg_s[:], in_=sgate_pre.rearrange("(h p) k -> p h k", p=P))
-            nc.sync.dma_start(out=gb_t[:], in_=gb0.rearrange("t k -> (t k)").partition_broadcast(P))
-            nc.sync.dma_start(out=gb_s[:], in_=gbs.partition_broadcast(P))
+            if not CFG["gb_by_pe"]:
+                nc.sync.dma_start(out=gate_bias["t"], in_=gb0.rearrange("t k -> (t k)").partition_broadcast(P))
+                nc.sync.dma_start(out=gate_bias["s"], in_=gbs.partition_broadcast(P))
 
         dall = const.tile([P, BC, NSLOT, NB], F32, name="dall")
         spread = {}
 
         def build_gates():
             gl = const.tile([P, 2, 104], F32, name="gl")
+            bias_t, bias_s = gate_bias["t"], gate_bias["s"]
             nc.vector.tensor_tensor(
-                out=gl[:, :, 0:64], in0=lg_t[:], in1=gb_t[:].unsqueeze(1).to_broadcast([P, 2, 64]), op=ALU.add
+                out=gl[:, :, 0:64], in0=lg_t[:], in1=bias_t.unsqueeze(1).to_broadcast([P, 2, 64]), op=ALU.add
             )
             nc.vector.tensor_tensor(
-                out=gl[:, :, 64:104], in0=lg_s[:], in1=gb_s[:].unsqueeze(1).to_broadcast([P, 2, 40]), op=ALU.add
+                out=gl[:, :, 64:104], in0=lg_s[:], in1=bias_s.unsqueeze(1).to_broadcast([P, 2, 40]), op=ALU.add
             )
             task_view = gl[:, :, 0:64].rearrange("p h (t k) -> p h t k", t=T)
             share_view = gl[:, :, 64:104]
@@ -401,8 +416,6 @@ def tile_plelayer_pa_kernel(
                 if CFG["tail"] and at >= t_last:
                     at = max(t_last + (at - t_last) // 2, at - CFG["tail"])
                 gate_at.setdefault(at, []).append((i, q))
-        if CFG["tail"]:
-            o_store = o_store - CFG["tail"]
         with tc.manual_schedule(engines=pins):
             for tau in range(-16, 4 * n_units + 8 + o_store):
                 s, q = divmod(tau, 4)
@@ -432,6 +445,11 @@ def tile_plelayer_pa_kernel(
                     widen(s + 3, q)
                 ti, tq = divmod(tau - o_turn, 4)
                 si, sq = divmod(tau - o_store, 4)
+                if CFG["tail"]:
+                    if si == n_units - 1:
+                        si = -1
+                    if divmod(tau - o_store + CFG["tail"], 4)[0] == n_units - 1:
+                        si, sq = divmod(tau - o_store + CFG["tail"], 4)
                 wide = expert_passes(s, q) if live(s) else []
                 due = [iq for iq in gate_at.get(tau, ())]
                 if s >= n_units and tau < 4 * (n_units - 1) + o_store + 3 and CFG["tail_fill"]:

@@ -26,7 +26,7 @@ SLAB = P * E
 NSLOT = 13
 GROUP_ORDER = (T, 0, 1, 2, 3)
 TURN_ON_VECTOR = (0, 2)
-CFG = {"vkind": None, "vwiden": None, "repeats": (0, 0, 1), "run": 8, "bufs": {"hs": 3, "res": 3}, "pin": "PE", "o_turn": 4, "o_gate": 8, "o_store": 12, "early_gates": False, "tail": 0, "repeat_rule": "heavy", "q_same_step": False, "bytes_first": False, "tail_fill": (), "copy_order": "jh", "gb_by_pe": True}
+CFG = {"vkind": None, "vwiden": None, "repeats": (0, 0, 1), "run": 8, "bufs": {"hs": 3, "res": 3}, "pin": "PE", "o_turn": 4, "o_gate": 8, "o_store": 12, "early_gates": False, "tail": 0, "repeat_rule": "heavy", "q_same_step": False, "bytes_first": False, "tail_fill": (), "copy_order": "jh", "gb_by_pe": True, "one_bias_load": True, "o_load": 4, "early_vwiden": (), "late_task_bias": True, "x_after_slab": True}
 ACC = 6
 UB = 32
 NF = P // UB
@@ -55,22 +55,26 @@ def tile_plelayer_pa_kernel(
         make_identity(nc, ident[:])
 
         x_sb = const.tile([P, 2, D], BF16, name="x_sb")
-        nc.sync.dma_start(out=x_sb[:], in_=x.rearrange("(h p) d -> p h d", p=P))
         sc = const.tile([P, PACK], F32, name="sc")
-
-        xt = psum.tile([P, 2, 2, P], F32, name="xt", tag="tp", bufs=nbufs("tp", 2))
-        for h in range(2):
-            words = x_sb[:, h, :].bitcast(F32)
-            for w in range(2):
-                nc.tensor.transpose(xt[:, h, w, :], words[:, w : D // 2 : 2], ident[:])
         xg = const.tile([P, PACK * B], BF16, name="xg", align_bytes=64)
-        nc.vector.tensor_copy(
-            out=xg[:].bitcast(F32).rearrange("p (h r w) -> p h r w", h=2, w=2),
-            in_=xt[:].rearrange("p h w r -> p h r w"),
-        )
         xcodes = const.tile([P, B], U32, name="xcodes", align_bytes=64)
         xscl = const.tile([P, B], U8, name="xscl", align_bytes=64)
-        nc.vector.quantize_mx(out=xcodes[:].bitcast(FP8X4), scales=xscl[:], in_=xg[:])
+
+        def prepare_x():
+            nc.sync.dma_start(out=x_sb[:], in_=x.rearrange("(h p) d -> p h d", p=P))
+            xt = psum.tile([P, 2, 2, P], F32, name="xt", tag="tp", bufs=nbufs("tp", 2))
+            for h in range(2):
+                words = x_sb[:, h, :].bitcast(F32)
+                for w in range(2):
+                    nc.tensor.transpose(xt[:, h, w, :], words[:, w : D // 2 : 2], ident[:])
+            nc.vector.tensor_copy(
+                out=xg[:].bitcast(F32).rearrange("p (h r w) -> p h r w", h=2, w=2),
+                in_=xt[:].rearrange("p h w r -> p h r w"),
+            )
+            nc.vector.quantize_mx(out=xcodes[:].bitcast(FP8X4), scales=xscl[:], in_=xg[:])
+
+        if not CFG["x_after_slab"]:
+            prepare_x()
 
         bias_rows = const.tile([P, UB * E], BF16, name="bias_rows")
         bias_sorted = const.tile([P, EL, P], F32, name="bias_sorted")
@@ -89,11 +93,26 @@ def tile_plelayer_pa_kernel(
             )
 
             nc.sync.dma_start(out=bias_bf[:, T, :, :], in_=ebs0.rearrange("(c p) e -> p c e", p=P))
-            for t in range(T):
-                nc.sync.dma_start(out=bias_bf[:, t, :, :], in_=eb0[t].rearrange("(c p) e -> p c e", p=P))
+            if not CFG["late_task_bias"]:
+                load_task_biases()
+
+        def load_task_biases():
+            if CFG["one_bias_load"]:
+                nc.sync.dma_start(
+                    out=bias_bf[:, 0:T, :, :].rearrange("p t c e -> p (t c) e"), in_=eb0.rearrange("t (c p) e -> p (t c) e", p=P)
+                )
+            else:
+                for t in range(T):
+                    nc.sync.dma_start(out=bias_bf[:, t, :, :], in_=eb0[t].rearrange("(c p) e -> p c e", p=P))
+
+        def cast_task_biases():
+            nc.gpsimd.tensor_copy(out=bias_u[:, 0:T, :, :], in_=bias_bf[:, 0:T, :, :])
 
         def cast_biases():
-            nc.gpsimd.tensor_copy(out=bias_u[:], in_=bias_bf[:])
+            if CFG["late_task_bias"]:
+                nc.gpsimd.tensor_copy(out=bias_u[:, T, :, :], in_=bias_bf[:, T, :, :])
+            else:
+                nc.gpsimd.tensor_copy(out=bias_u[:], in_=bias_bf[:])
             nc.gpsimd.tensor_copy(
                 out=bias_sorted[:].rearrange("r l (h u) -> r l h u", h=EH),
                 in_=bias_rows[:].rearrange("r (u h l) -> r l h u", h=EH, l=EL),
@@ -231,7 +250,7 @@ def tile_plelayer_pa_kernel(
         def widen(i, j):
             if units[i][1] == T:
                 return
-            if j == 0:
+            if i not in planes:
                 planes[i] = stage.tile([P, PACK, SLAB], BF16, name="planes", tag="planes", bufs=nbufs("planes", 3))
             if vwiden(i, j):
                 nc.vector.tensor_scalar(
@@ -426,8 +445,11 @@ def tile_plelayer_pa_kernel(
                     if CFG["bytes_first"] and s == -4:
                         load_scale()
                         load(1)
-                    if live(s + 4) and not (CFG["bytes_first"] and s + 4 == 1):
-                        load(s + 4)
+                    for i in range(n_units):
+                        if (i - 4 if i < 5 else i - CFG["o_load"]) == s and not (CFG["bytes_first"] and i == 1):
+                            load(i)
+                    if s == -4 and CFG["x_after_slab"]:
+                        prepare_x()
                     if s == -4 and not CFG["bytes_first"]:
                         load_scale()
                     if s == -3:
@@ -437,12 +459,17 @@ def tile_plelayer_pa_kernel(
                         load_gates()
                     if s == -1:
                         turn_biases()
+                        if CFG["late_task_bias"]:
+                            load_task_biases()
+                            cast_task_biases()
                 if live(s + 2) and q % 2 == 0:
                     interleave(s + 2, q // 2)
                     if s + 2 == 0 and not CFG["q_same_step"]:
                         quantize(0, q // 2)
-                if live(s + 3):
+                if live(s + 3) and not (s + 3 in CFG["early_vwiden"] and vwiden(s + 3, q)):
                     widen(s + 3, q)
+                if s + 4 in CFG["early_vwiden"] and vwiden(s + 4, q):
+                    widen(s + 4, q)
                 ti, tq = divmod(tau - o_turn, 4)
                 si, sq = divmod(tau - o_store, 4)
                 if CFG["tail"]:

from contextlib import ExitStack

import concourse.mybir as mybir
from concourse.masks import make_identity

T, B, D, U, E = 4, 256, 512, 512, 8
FLOPS = 2 * B * D * (T + 1) * U * E

F32 = mybir.dt.float32
BF16 = mybir.dt.bfloat16
U32 = mybir.dt.uint32
U8 = mybir.dt.uint8
FP8 = mybir.dt.float8_e4m3fn
FP8X4 = mybir.dt.float8_e4m3fn_x4
ACT = mybir.ActivationFunctionType
ALU = mybir.AluOpType
AX = mybir.AxisListType

P = 128
PACK = 4
NG = T + 1
UC = U // P
NB = 16
BC = B // NB
SLAB = P * E
NSLOT = 13
GROUP_ORDER = (T, 0, 1, 2, 3)
TURN_ON_VECTOR = (0, 2)
CFG = {"vkind": None, "vwiden": None, "repeats": (0, 0, 1), "run": 8, "bufs": {"hs": 3, "res": 3}, "pin": "PE", "o_turn": 4, "o_gate": 8, "o_store": 12, "early_gates": False, "tail": 0, "repeat_rule": "heavy", "q_same_step": False, "bytes_first": False, "tail_fill": (), "copy_order": "jh", "gb_by_pe": True, "one_bias_load": True, "o_load": 4, "early_vwiden": (), "late_task_bias": True, "x_after_slab": True}
ACC = 6
UB = 32
NF = P // UB
EH = 4
EL = 2


def tile_plelayer_pa_kernel(
    tc, x, ews0, ebs0, ew0_bytes, ew0_scale, eb0, gate_pre0, gb0, sgate_pre, gbs, out_0, out_1
):
    nc = tc.nc

    def nbufs(tag, n):
        return CFG["bufs"].get(tag, n)

    with ExitStack() as ctx:
        const = ctx.enter_context(tc.tile_pool(name="const", bufs=1))
        stage = ctx.enter_context(tc.tile_pool(name="stage", bufs=2))
        psum = ctx.enter_context(tc.psum_pool(name="psum", bufs=2))

        warm = const.tile([P, 1], F32, name="warm")
        nc.vector.memset(warm[:], 0.0)
        nc.scalar.activation(out=warm[:], in_=warm[:], func=ACT.Exp)

        ident = const.tile([P, P], F32, name="ident")
        make_identity(nc, ident[:])

        x_sb = const.tile([P, 2, D], BF16, name="x_sb")
        sc = const.tile([P, PACK], F32, name="sc")
        xg = const.tile([P, PACK * B], BF16, name="xg", align_bytes=64)
        xcodes = const.tile([P, B], U32, name="xcodes", align_bytes=64)
        xscl = const.tile([P, B], U8, name="xscl", align_bytes=64)

        def prepare_x():
            nc.sync.dma_start(out=x_sb[:], in_=x.rearrange("(h p) d -> p h d", p=P))
            xt = psum.tile([P, 2, 2, P], F32, name="xt", tag="tp", bufs=nbufs("tp", 2))
            for h in range(2):
                words = x_sb[:, h, :].bitcast(F32)
                for w in range(2):
                    nc.tensor.transpose(xt[:, h, w, :], words[:, w : D // 2 : 2], ident[:])
            nc.vector.tensor_copy(
                out=xg[:].bitcast(F32).rearrange("p (h r w) -> p h r w", h=2, w=2),
                in_=xt[:].rearrange("p h w r -> p h r w"),
            )
            nc.vector.quantize_mx(out=xcodes[:].bitcast(FP8X4), scales=xscl[:], in_=xg[:])

        if not CFG["x_after_slab"]:
            prepare_x()

        bias_rows = const.tile([P, UB * E], BF16, name="bias_rows")
        bias_sorted = const.tile([P, EL, P], F32, name="bias_sorted")
        bias_q = const.tile([P, EL, P], F32, name="bias_q")
        nc.vector.memset(bias_rows[:], 0.0)
        bias_bf = const.tile([P, NG, UC, E], BF16, name="bias_bf")
        bias_u = const.tile([P, NG, UC, E], F32, name="bias_u")

        def load_scale():
            nc.sync.dma_start(out=sc[:], in_=ew0_scale.rearrange("o (p j) a b -> p (o j a b)", j=PACK))

        def load_biases():
            nc.sync.dma_start(out=bias_rows[0 : T * UC * NF, :], in_=eb0.rearrange("t (r u) e -> (t r) (u e)", u=UB))
            nc.sync.dma_start(
                out=bias_rows[T * UC * NF : NG * UC * NF, :], in_=ebs0.rearrange("(r u) e -> r (u e)", u=UB)
            )

            nc.sync.dma_start(out=bias_bf[:, T, :, :], in_=ebs0.rearrange("(c p) e -> p c e", p=P))
            if not CFG["late_task_bias"]:
                load_task_biases()

        def load_task_biases():
            if CFG["one_bias_load"]:
                nc.sync.dma_start(
                    out=bias_bf[:, 0:T, :, :].rearrange("p t c e -> p (t c) e"), in_=eb0.rearrange("t (c p) e -> p (t c) e", p=P)
                )
            else:
                for t in range(T):
                    nc.sync.dma_start(out=bias_bf[:, t, :, :], in_=eb0[t].rearrange("(c p) e -> p c e", p=P))

        def cast_task_biases():
            nc.gpsimd.tensor_copy(out=bias_u[:, 0:T, :, :], in_=bias_bf[:, 0:T, :, :])

        def cast_biases():
            if CFG["late_task_bias"]:
                nc.gpsimd.tensor_copy(out=bias_u[:, T, :, :], in_=bias_bf[:, T, :, :])
            else:
                nc.gpsimd.tensor_copy(out=bias_u[:], in_=bias_bf[:])
            nc.gpsimd.tensor_copy(
                out=bias_sorted[:].rearrange("r l (h u) -> r l h u", h=EH),
                in_=bias_rows[:].rearrange("r (u h l) -> r l h u", h=EH, l=EL),
            )

        def turn_biases():
            bt = psum.tile([P, EL, P], F32, name="bt", tag="tp", bufs=nbufs("tp", 2))
            for l in range(EL):
                nc.tensor.transpose(bt[:, l, :], bias_sorted[:, l, :], ident[:])
            nc.scalar.copy(out=bias_q[:], in_=bt[:])

        lg_t = const.tile([P, 2, 64], BF16, name="lg_t")
        lg_s = const.tile([P, 2, 40], BF16, name="lg_s")
        gate_bias = {}
        if CFG["gb_by_pe"]:
            gb_row = const.tile([P, 104], BF16, name="gb_row")
            ones = const.tile([P, P], BF16, name="ones")
            nc.vector.memset(gb_row[:], 0.0)
            nc.vector.memset(ones[:], 1.0)
            nc.sync.dma_start(out=gb_row[0:1, 0:64], in_=gb0.rearrange("(o t) k -> o (t k)", o=1))
            nc.sync.dma_start(out=gb_row[0:1, 64:104], in_=gbs.rearrange("(o k) -> o k", o=1))
            gbp = psum.tile([P, 104], F32, name="gbp", tag="tp", bufs=nbufs("tp", 2))
            nc.tensor.matmul(out=gbp[:], lhsT=ones[:], rhs=gb_row[:], start=True, stop=True)
            gate_bias["t"], gate_bias["s"] = gbp[:, 0:64], gbp[:, 64:104]
        else:
            gb_t = const.tile([P, 64], BF16, name="gb_t")
            gb_s = const.tile([P, 40], BF16, name="gb_s")
            gate_bias["t"], gate_bias["s"] = gb_t[:], gb_s[:]

        def load_gates():
            for h in range(2):
                nc.sync.dma_start(
                    out=lg_t[:, h, :].rearrange("p (t k) -> p t k", t=T),
                    in_=gate_pre0[:, h * P : (h + 1) * P, :].rearrange("t p k -> p t k"),
                )
            nc.sync.dma_start(out=lg_s[:], in_=sgate_pre.rearrange("(h p) k -> p h k", p=P))
            if not CFG["gb_by_pe"]:
                nc.sync.dma_start(out=gate_bias["t"], in_=gb0.rearrange("t k -> (t k)").partition_broadcast(P))
                nc.sync.dma_start(out=gate_bias["s"], in_=gbs.partition_broadcast(P))

        dall = const.tile([P, BC, NSLOT, NB], F32, name="dall")
        spread = {}

        def build_gates():
            gl = const.tile([P, 2, 104], F32, name="gl")
            bias_t, bias_s = gate_bias["t"], gate_bias["s"]
            nc.vector.tensor_tensor(
                out=gl[:, :, 0:64], in0=lg_t[:], in1=bias_t.unsqueeze(1).to_broadcast([P, 2, 64]), op=ALU.add
            )
            nc.vector.tensor_tensor(
                out=gl[:, :, 64:104], in0=lg_s[:], in1=bias_s.unsqueeze(1).to_broadcast([P, 2, 40]), op=ALU.add
            )
            task_view = gl[:, :, 0:64].rearrange("p h (t k) -> p h t k", t=T)
            share_view = gl[:, :, 64:104]
            mx = const.tile([P, 2, 5], F32, name="mx")
            nc.vector.tensor_reduce(out=mx[:, :, 0:4], in_=task_view, axis=AX.X, op=ALU.max)
            nc.vector.tensor_reduce(out=mx[:, :, 4:5], in_=share_view, axis=AX.X, op=ALU.max)
            nc.vector.tensor_tensor(
                out=task_view, in0=task_view, in1=mx[:, :, 0:4].unsqueeze(3).to_broadcast([P, 2, T, 16]), op=ALU.subtract
            )
            nc.vector.tensor_tensor(
                out=share_view, in0=share_view, in1=mx[:, :, 4:5].to_broadcast([P, 2, 40]), op=ALU.subtract
            )
            nc.scalar.activation(out=gl[:], in_=gl[:], func=ACT.Exp)
            sm = const.tile([P, 2, 5], F32, name="sm")
            nc.vector.tensor_reduce(out=sm[:, :, 0:4], in_=task_view, axis=AX.X, op=ALU.add)
            nc.vector.tensor_reduce(out=sm[:, :, 4:5], in_=share_view, axis=AX.X, op=ALU.add)
            rc = const.tile([P, 2, 5], F32, name="rc")
            nc.vector.reciprocal(out=rc[:], in_=sm[:])
            nc.vector.tensor_tensor(
                out=task_view, in0=task_view, in1=rc[:, :, 0:4].unsqueeze(3).to_broadcast([P, 2, T, 16]), op=ALU.mult
            )
            nc.vector.tensor_tensor(
                out=share_view, in0=share_view, in1=rc[:, :, 4:5].to_broadcast([P, 2, 40]), op=ALU.mult
            )
            mask = const.tile([P, NB], F32, name="mask")
            nc.vector.tensor_reduce(
                out=mask[:], in_=ident[:].rearrange("p (c b) -> p b c", b=NB), axis=AX.X, op=ALU.add
            )
            mask4 = mask[:].unsqueeze(1).unsqueeze(1).to_broadcast([P, T, E, NB])
            for h in range(2):
                fm = const.tile([P, NSLOT, E, NB], F32, name="fm", tag="fm", bufs=2)
                spread[h] = fm
                halves = gl[:, h, 0:64].rearrange("p (t s e) -> p t s e", t=T, s=2)
                own = halves[:, :, 0, :].unsqueeze(3).to_broadcast([P, T, E, NB])
                shared = halves[:, :, 1, :].unsqueeze(3).to_broadcast([P, T, E, NB])
                sh_t = gl[:, h, 64:96].rearrange("p (t e) -> p t e", t=T).unsqueeze(3).to_broadcast([P, T, E, NB])
                sh_s = gl[:, h, 96:104].unsqueeze(2).to_broadcast([P, E, NB])
                nc.vector.tensor_tensor(out=fm[:, 0:4, :, :], in0=shared, in1=mask4, op=ALU.mult)
                nc.vector.tensor_tensor(
                    out=fm[:, 4, :, :], in0=sh_s, in1=mask[:].unsqueeze(1).to_broadcast([P, E, NB]), op=ALU.mult
                )
                nc.vector.tensor_tensor(out=fm[:, 5:NSLOT:2, :, :], in0=own, in1=mask4, op=ALU.mult)
                nc.vector.tensor_tensor(out=fm[:, 6:NSLOT:2, :, :], in0=sh_t, in1=mask4, op=ALU.mult)

        def turn_gates(h, s0):
            n = min(4, NSLOT - s0)
            dps = psum.tile([P, 4, P], F32, name="dps", tag="tp", bufs=nbufs("tp", 2))
            for i in range(n):
                nc.tensor.transpose(
                    dps[:, i, :], spread[h][:, s0 + i, :, :].rearrange("p e b -> p (e b)"), ident[:]
                )
            nc.scalar.copy(
                out=dall[:, 8 * h : 8 * h + 8, s0 : s0 + n, :].rearrange("p c s b -> p s c b"),
                in_=dps[:, 0:n, :].rearrange("p s (c b) -> p s c b", b=NB),
            )

        units = [(uc, g) for uc in range(UC) for g in GROUP_ORDER]
        n_units = len(units)

        def vkind(i):
            if CFG["vkind"] is not None:
                return i in CFG["vkind"]
            return units[i][1] in TURN_ON_VECTOR

        def vwiden(i, j):
            if CFG["vwiden"] is not None:
                return j in CFG["vwiden"][i]
            return j == 3 or (j > 0 and not vkind(i))
        raw, planes, grouped, codes, scales, relu_out = {}, {}, {}, {}, {}, {}
        turned, sums, acc, banks = {}, {}, {}, {}

        def load(i):
            uc, g = units[i]
            cols = slice(uc * SLAB, (uc + 1) * SLAB)
            if g == T:
                pl = stage.tile([P, PACK, SLAB], BF16, name="planes", tag="planes", bufs=nbufs("planes", 3))
                nc.sync.dma_start(out=pl[:], in_=ews0.rearrange("(p j) u e -> p j (u e)", j=PACK)[:, :, cols])
                planes[i] = pl
            else:
                wb = stage.tile([P, PACK, SLAB], U8, name="wbytes", tag="wbytes", bufs=nbufs("wbytes", 3))
                nc.sync.dma_start(out=wb[:], in_=ew0_bytes[g].rearrange("(p j) u e -> p j (u e)", j=PACK)[:, :, cols])
                raw[i] = wb

        def widen(i, j):
            if units[i][1] == T:
                return
            if i not in planes:
                planes[i] = stage.tile([P, PACK, SLAB], BF16, name="planes", tag="planes", bufs=nbufs("planes", 3))
            if vwiden(i, j):
                nc.vector.tensor_scalar(
                    out=planes[i][:, j, :],
                    in0=raw[i][:, j, :].bitcast(FP8),
                    scalar1=sc[:, j : j + 1],
                    scalar2=None,
                    op0=ALU.mult,
                )
            else:
                nc.scalar.activation(
                    out=planes[i][:, j, :], in_=raw[i][:, j, :].bitcast(FP8), func=ACT.Copy, scale=sc[:, j : j + 1]
                )

        def interleave(i, half):
            if half == 0:
                grouped[i] = stage.tile([P, PACK * SLAB], BF16, name="grp", tag="grp", bufs=nbufs("grp", 2), align_bytes=64)
            if vkind(i):
                dst = grouped[i][:].rearrange("p (l f h u j) -> p l f u h j", l=EL, f=NF, h=EH, j=PACK)
                src = planes[i][:].rearrange("p j (f u h l) -> p l f u h j", f=NF, h=EH, l=EL)
            else:
                dst = grouped[i][:].rearrange("p (l h u j) -> p l u h j", l=EL, h=EH, j=PACK)
                src = planes[i][:].rearrange("p j (u l h) -> p l u h j", l=EL, h=EH)
            if CFG["copy_order"] == "jh":
                if vkind(i):
                    dst, src = dst.rearrange("p l f u h j -> p l f u j h"), src.rearrange("p l f u h j -> p l f u j h")
                else:
                    dst, src = dst.rearrange("p l u h j -> p l u j h"), src.rearrange("p l u h j -> p l u j h")
            nc.vector.tensor_copy(out=dst[:, half], in_=src[:, half])

        def quantize(i, half):
            if half == 0:
                codes[i] = stage.tile([P, SLAB], U32, name="wcodes", tag="wcodes", bufs=nbufs("wcodes", 3), align_bytes=64)
                scales[i] = stage.tile([P, SLAB], U8, name="wscl", tag="wscl", bufs=nbufs("wscl", 3), align_bytes=64)
            cols = slice(half * SLAB // 2, (half + 1) * SLAB // 2)
            nc.vector.quantize_mx(
                out=codes[i][:, cols].bitcast(FP8X4),
                scales=scales[i][:, cols],
                in_=grouped[i][:, half * 2 * SLAB : (half + 1) * 2 * SLAB],
            )

        def mx_pass(out, cd, sl, e, rhs, rhs_scale):
            cols = slice(e * P, (e + 1) * P)
            nc.tensor.matmul_mx(
                out=out,
                lhsT=cd[:, cols].bitcast(FP8X4),
                lhsT_scale=sl[:, cols],
                rhs=rhs.bitcast(FP8X4),
                rhs_scale=rhs_scale,
                start=True,
                stop=True,
            )

        def expert_passes(i, q):
            cd, sl = codes[i], scales[i]
            if q == 0:
                relu_out[i] = stage.tile([P, BC, P], F32, name="hs", tag="hs", bufs=nbufs("hs", 2), align_bytes=64)
            e0 = 2 * q
            z = psum.tile([P, 2, B], F32, name="z", tag="z", bufs=nbufs("z", 3))
            banks[i] = z
            ops = []
            pattern = CFG["repeats"]
            if live(i - 1) and CFG["repeat_rule"] == ("heavy" if vkind(i - 1) else "light"):
                pattern = (0, 1)
            for k in pattern:
                ops.append(lambda k=k: mx_pass(z[:, k, :], cd, sl, e0 + k, xcodes[:], xscl[:]))
            return ops

        def filler_passes(q):
            cd, sl = codes[n_units - 1], scales[n_units - 1]
            z = psum.tile([P, 2, B], F32, name="z", tag="z", bufs=nbufs("z", 3))
            ops = []
            for k in CFG["tail_fill"]:
                ops.append(lambda k=k: mx_pass(z[:, k, :], cd, sl, 2 * q + k, xcodes[:], xscl[:]))
            return ops

        def expert_relu(i, q):
            uc, g = units[i]
            for k in range(2):
                if vkind(i):
                    l, f = divmod(2 * q + k, NF)
                    row = g * UC * NF + uc * NF + f
                    dest = relu_out[i][:].rearrange("p c (f l b) -> p c f l b", f=NF, l=EL)[:, :, f, l, :]
                    bias = bias_q[:, l, row : row + 1]
                else:
                    e = 2 * q + k
                    dest = relu_out[i][:].rearrange("p c (e b) -> p c e b", e=E)[:, :, e, :]
                    bias = bias_u[:, g, uc, e : e + 1]
                nc.scalar.activation(
                    out=dest,
                    in_=banks[i][:, k, :].rearrange("p (c b) -> p c b", b=NB),
                    func=ACT.Relu,
                    bias=bias,
                    scale=1.0,
                )

        def turn(i, q):
            if q == 0:
                turned[i] = stage.tile([P, BC, P], F32, name="ht", tag="ht", bufs=nbufs("ht", 3), align_bytes=64)
            hs, ht = relu_out[i], turned[i]
            if vkind(i):
                nc.vector.transpose(
                    out=ht[:, 4 * q : 4 * q + 4, :].rearrange("p c u -> p (c u)"),
                    in_=hs[:, 4 * q : 4 * q + 4, :].rearrange("p c k -> p (c k)"),
                )
            else:
                tp = psum.tile([P, 4, P], F32, name="tp", tag="tp", bufs=nbufs("tp", 2))
                for k in range(4):
                    nc.tensor.transpose(tp[:, k, :], hs[:, 4 * q + k, :], ident[:])
                nc.scalar.copy(out=ht[:, 4 * q : 4 * q + 4, :], in_=tp[:])

        def gate_pass(out, ht, bc, s0, s1, start, stop):
            nc.tensor.matmul(out=out, lhsT=ht[:, bc, :], rhs=dall[:, bc, s0:s1, :], start=start, stop=stop)

        def gate_passes(i, q):
            uc, g = units[i]
            ht = turned[i]
            ops = []
            for bc in range(4 * q, 4 * q + 4):
                bank, k = divmod(bc, ACC)
                if g == T and k == 0:
                    acc[bank] = psum.tile([P, 512], F32, name="acc%d" % bank, tag="acc%d" % bank, bufs=1)
                a = acc[bank][:, 0 : ACC * NG * NB].rearrange("p (k j b) -> p k j b", j=NG, b=NB)
                if g == T:
                    ops.append(lambda a=a, k=k, bc=bc: gate_pass(a[:, k, :, :], ht, bc, 0, NG, k == 0, False))
                else:
                    last = g == T - 1 and (k == ACC - 1 or bc == BC - 1)
                    ops.append(
                        lambda a=a, k=k, bc=bc, last=last: gate_pass(
                            a[:, k, g : NG : T - g, :], ht, bc, 5 + 2 * g, 7 + 2 * g, False, last
                        )
                    )
            return ops

        def acc_copy(i, q):
            uc, g = units[i]
            if g != T - 1 or q == 0:
                return
            bank = q - 1
            if bank == 0:
                sums[uc] = stage.tile([P, NG, B], F32, name="ot", tag="ot", bufs=nbufs("ot", 2))
            n = min(ACC, BC - ACC * bank)
            a = acc[bank][:, 0 : ACC * NG * NB].rearrange("p (k j b) -> p k j b", j=NG, b=NB)
            nc.scalar.copy(
                out=sums[uc][:, :, ACC * NB * bank : ACC * NB * bank + n * NB].rearrange("p j (k b) -> p k j b", b=NB),
                in_=a[:, 0:n, :, :],
            )

        def store(i, r):
            uc, g = units[i]
            if g != T - 1:
                return
            ot = sums[uc]
            ucols = slice(uc * P, (uc + 1) * P)
            done = ((0, 1), (2, 3), (T,))[r]
            n = len(done)
            fp = psum.tile([P, 2, 2, P], F32, name="fp", tag="tp", bufs=nbufs("tp", 2))
            for k in range(n):
                for h in range(2):
                    nc.tensor.transpose(fp[:, k, h, :], ot[:, done[k], h * P : (h + 1) * P], ident[:])
            res = stage.tile([P, 2, 2, P], F32, name="res", tag="res", bufs=nbufs("res", 2))
            nc.scalar.copy(out=res[:, 0:n, :, :], in_=fp[:, 0:n, :, :])
            for k in range(n):
                dest = out_1 if done[k] == T else out_0[done[k]]
                nc.sync.dma_start(out=dest.rearrange("(h p) u -> p h u", p=P)[:, :, ucols], in_=res[:, k, :, :])

        def live(i):
            return 0 <= i < n_units

        pins = {
            "PE": {mybir.EngineType.PE},
            "PE+ACT": {mybir.EngineType.PE, mybir.EngineType.Activation},
            "PE+DVE": {mybir.EngineType.PE, mybir.EngineType.DVE},
            "PE+ACT+DVE": {mybir.EngineType.PE, mybir.EngineType.Activation, mybir.EngineType.DVE},
        }[CFG["pin"]]
        o_turn, o_gate, o_store = CFG["o_turn"], CFG["o_gate"], CFG["o_store"]
        gate_at = {}
        t_last = 4 * (n_units - 1)
        for i in range(n_units):
            for q in range(4):
                at = 4 * i + q + o_gate
                if CFG["tail"] and at >= t_last:
                    at = max(t_last + (at - t_last) // 2, at - CFG["tail"])
                gate_at.setdefault(at, []).append((i, q))
        with tc.manual_schedule(engines=pins):
            for tau in range(-16, 4 * n_units + 8 + o_store):
                s, q = divmod(tau, 4)
                if tau == -16 and CFG["early_gates"]:
                    load_gates()
                    build_gates()
                if q == 0:
                    if CFG["bytes_first"] and s == -4:
                        load_scale()
                        load(1)
                    for i in range(n_units):
                        if (i - 4 if i < 5 else i - CFG["o_load"]) == s and not (CFG["bytes_first"] and i == 1):
                            load(i)
                    if s == -4 and CFG["x_after_slab"]:
                        prepare_x()
                    if s == -4 and not CFG["bytes_first"]:
                        load_scale()
                    if s == -3:
                        load_biases()
                        cast_biases()
                    if s == -2 and not CFG["early_gates"]:
                        load_gates()
                    if s == -1:
                        turn_biases()
                        if CFG["late_task_bias"]:
                            load_task_biases()
                            cast_task_biases()
                if live(s + 2) and q % 2 == 0:
                    interleave(s + 2, q // 2)
                    if s + 2 == 0 and not CFG["q_same_step"]:
                        quantize(0, q // 2)
                if live(s + 3) and not (s + 3 in CFG["early_vwiden"] and vwiden(s + 3, q)):
                    widen(s + 3, q)
                if s + 4 in CFG["early_vwiden"] and vwiden(s + 4, q):
                    widen(s + 4, q)
                ti, tq = divmod(tau - o_turn, 4)
                si, sq = divmod(tau - o_store, 4)
                if CFG["tail"]:
                    if si == n_units - 1:
                        si = -1
                    if divmod(tau - o_store + CFG["tail"], 4)[0] == n_units - 1:
                        si, sq = divmod(tau - o_store + CFG["tail"], 4)
                wide = expert_passes(s, q) if live(s) else []
                due = [iq for iq in gate_at.get(tau, ())]
                if s >= n_units and tau < 4 * (n_units - 1) + o_store + 3 and CFG["tail_fill"]:
                    wide = filler_passes(q)
                thin = []
                for gi, gq in due:
                    thin.extend(gate_passes(gi, gq))
                for n in range(max(len(thin), len(wide))):
                    if n < len(thin):
                        thin[n]()
                    if n < len(wide):
                        wide[n]()
                if live(s):
                    expert_relu(s, q)
                for gi, gq in due:
                    acc_copy(gi, gq)
                if live(ti):
                    if vkind(ti) or CFG["run"] == 4:
                        turn(ti, tq)
                    elif tq % 2 == 1:
                        turn(ti, tq - 1)
                        turn(ti, tq)
                if CFG["q_same_step"]:
                    if live(s + 2) and q % 2 == 1:
                        quantize(s + 2, q // 2)
                elif live(s + 1) and s + 1 > 0 and q % 2 == 1:
                    quantize(s + 1, q // 2)
                if s in (1, 2):
                    turn_gates(q % 2, 8 * (s - 1) + 4 * (q // 2))
                if live(si) and sq < 3:
                    store(si, sq)
                if s == -2 and q == 3 and not CFG["early_gates"]:
                    build_gates()
